import numpy as np
import ml_dtypes


def mxq(x, axis, fmt="e4m3"):
    dtype, down = {"e4m3": (ml_dtypes.float8_e4m3fn, 7), "e5m2": (ml_dtypes.float8_e5m2, 14)}[fmt]
    v = np.moveaxis(np.asarray(x, np.float32).astype(ml_dtypes.bfloat16).astype(np.float64), axis, -1)
    blocks = v.reshape(v.shape[:-1] + (-1, 32))
    amax = np.abs(blocks).max(-1, keepdims=True)
    byte = np.maximum(np.where(amax > 0, np.frexp(amax)[1] - 1 + 127, 0) - down, 1)
    scale = np.exp2(byte - 127.0)
    codes = (blocks / scale).astype(np.float32).astype(dtype).astype(np.float64)
    return np.moveaxis((codes * scale).reshape(v.shape), -1, axis)


WIDE = False


def mx_kscale(k):
    if not WIDE:
        return np.ones(k)
    levels = np.array([10, -10, 5, -5, 0])
    if k % 512:
        return np.exp2(np.random.permutation(np.resize(levels, k // 32))).repeat(32)
    a = np.empty((k // 512, 16))
    for p in range(k // 512):
        a[p, :8] = np.random.permutation(np.resize(levels, 8))
        for g in range(8):
            far = levels[np.abs(levels - a[p, g]) >= 10]
            a[p, g + 8] = far[np.random.randint(len(far))]
    return np.exp2(a.ravel()).repeat(32)


BF16 = ml_dtypes.bfloat16


def bf(x):
    return np.asarray(x, np.float32).astype(BF16)


def f64(x):
    return np.asarray(x).astype(np.float64)


N, CIN, COUT, V, T, S = 1, 512, 128, 32, 128, 16
EPS = 1e-5
KG = S * V


def setup_inputs():
    r = np.random.standard_normal
    c = mx_kscale(CIN)
    g = mx_kscale(KG).reshape(S, V)
    return {"ada_A": bf(r((N, CIN, V, V)) * c[None, :, None, None]),
            "ada_w": bf(r((S, COUT, CIN)) / np.sqrt(CIN) / c),
            "ada_b": bf(r((S, COUT)) * 0.3),
            "PA": bf(r((S, V, V)) * 2.0 / np.sqrt(KG) * g[:, None, :]),
            "feat": bf(r((S, N, COUT, V, T)) / g[:, None, None, :, None]),
            "bn_gamma": bf(1.0 + 0.1 * r(COUT)),
            "bn_beta": bf(0.3 * r(COUT)),
            "bn_mean": bf(0.3 * r(COUT)),
            "bn_var": bf(np.abs(r(COUT)) + 1.0),
            "res": bf(r((N, COUT, V, T)) * 0.9)}


def reference(ada_A, ada_w, ada_b, PA, feat, bn_gamma, bn_beta, bn_mean, bn_var, res):
    wq = mxq(f64(ada_w).reshape(S * COUT, CIN), 1, "e4m3")
    aq = mxq(f64(ada_A).reshape(N, CIN, V * V), 1, "e4m3")
    adaA = (wq @ aq).reshape(N, S, COUT, V, V).transpose(1, 0, 2, 3, 4) + f64(ada_b)[:, None, :, None, None]
    A_full = adaA * f64(PA)[:, None, None, :, :]
    Ag = A_full.transpose(1, 2, 3, 0, 4).reshape(N, COUT, V, KG)
    Fg = f64(feat).transpose(1, 2, 0, 3, 4).reshape(N, COUT, KG, T)
    y = mxq(Ag, 3, "e4m3") @ mxq(Fg, 2, "e4m3")
    scale = f64(bn_gamma) / np.sqrt(f64(bn_var) + EPS)
    z = (y - f64(bn_mean)[:, None, None]) * scale[:, None, None] + f64(bn_beta)[:, None, None]
    return np.maximum(z + f64(res), 0.0)

@@ -1,0 +1,394 @@
+from contextlib import ExitStack
+
+import concourse.mybir as mybir
+from concourse.masks import make_identity
+
+F32 = mybir.dt.float32
+BF16 = mybir.dt.bfloat16
+U32 = mybir.dt.uint32
+U8 = mybir.dt.uint8
+FP8X4 = mybir.dt.float8_e4m3fn_x4
+ALU = mybir.AluOpType
+ACT = mybir.ActivationFunctionType
+AX = mybir.AxisListType
+
+P = 128
+S, CIN, COUT, V, T = 16, 512, 128, 32, 128
+EPS = 1e-5
+FLOPS = 2 * S * COUT * CIN * V * V + 2 * COUT * V * S * V * T
+N_TILES = COUT // 4
+RAW_BUFS = 6
+TILES_T0, TILES_S1, TILES_T1, TILES_QG = 7, 6, 5, 2
+
+
+def evenly(i, n, total):
+    return (i + 1) * n // total > i * n // total
+
+
+def tile_multiscale_gcn_pa_kernel(
+    tc, ada_A, ada_w, ada_b, PA, feat, bn_gamma, bn_beta, bn_mean, bn_var, res, out
+):
+    nc = tc.nc
+    with ExitStack() as ctx:
+        const = ctx.enter_context(tc.tile_pool(name="const", bufs=1))
+        keep = ctx.enter_context(tc.tile_pool(name="keep", bufs=1))
+        big = ctx.enter_context(tc.tile_pool(name="big", bufs=1))
+        raw_pool = ctx.enter_context(tc.tile_pool(name="rawp", bufs=RAW_BUFS))
+        grp_pool = ctx.enter_context(tc.tile_pool(name="grpp", bufs=4))
+        res_pool = ctx.enter_context(tc.tile_pool(name="resp", bufs=4))
+        ps_m = ctx.enter_context(tc.psum_pool(name="psm", bufs=4))
+        ps_t = ctx.enter_context(tc.psum_pool(name="pst", bufs=4))
+        ctx.enter_context(tc.manual_schedule())
+
+        w_codes = keep.tile([P, S * COUT], U32, align_bytes=64)
+        w_scales = keep.tile([P, S * COUT], U8, align_bytes=64)
+        a_codes = keep.tile([P, V * V], U32, align_bytes=64)
+        a_scales = keep.tile([P, V * V], U8, align_bytes=64)
+        g_codes = keep.tile([P, COUT * V], U32, align_bytes=64)
+        g_scales = keep.tile([P, COUT * V], U8, align_bytes=64)
+        f_codes = keep.tile([P, COUT * T], U32, align_bytes=64)
+        f_scales = keep.tile([P, COUT * T], U8, align_bytes=64)
+
+        zrows = const.tile([P, P], BF16)
+        nc.vector.memset(zrows[:], 0.0)
+        sq = const.tile([P, 2], F32)
+        nc.vector.memset(sq[:], 1.0)
+        nc.scalar.sqrt(out=sq[:, 1:2], in_=sq[:, 0:1])
+        ident32 = const.tile([P, P], F32)
+        make_identity(nc, ident32[:])
+        identb = const.tile([P, P], BF16)
+        make_identity(nc, identb[:])
+        nc.scalar.dma_start(out=zrows[4:20, :], in_=ada_b)
+        nc.scalar.dma_start(out=zrows[3:4, :], in_=bn_var.unsqueeze(0))
+        nc.scalar.dma_start(out=zrows[0:1, :], in_=bn_gamma.unsqueeze(0))
+        nc.scalar.dma_start(out=zrows[1:2, :], in_=bn_beta.unsqueeze(0))
+        nc.scalar.dma_start(out=zrows[2:3, :], in_=bn_mean.unsqueeze(0))
+
+        a2 = ada_A.rearrange("n i v w -> (n i) (v w)")
+        raws = {}
+
+        def load(kind, n):
+            r = raw_pool.tile([P, 2048], BF16, tag="raw", name="raw")
+            raws[(kind, n)] = r
+            if kind == "a":
+                r3 = r[:].rearrange("q (t c) -> q t c", t=4)
+                nc.sync.dma_start(
+                    out=r3, in_=a2[:, 512 * n : 512 * n + 512].rearrange("(q t) c -> q t c", t=4)
+                )
+            elif kind == "w":
+                nc.sync.dma_start(
+                    out=r[:].rearrange("o (s i) -> o s i", s=4),
+                    in_=ada_w[4 * n : 4 * n + 4].rearrange("s o i -> o s i"),
+                )
+            else:
+                for c in range(4):
+                    nc.sync.dma_start(
+                        out=r[:, 512 * c : 512 * c + 512],
+                        in_=feat[:, 0, 4 * n + c].rearrange("s (q j) t -> s q (j t)", j=4),
+                    )
+
+        loads = [("a", 0), ("w", 0), ("w", 1), ("w", 2), ("f", 0), ("w", 3), ("f", 1), ("a", 1)]
+        loads.extend([("f", g) for g in range(2, N_TILES)])
+        state = {"loaded": 0, "next": 0, "quantised": 0}
+
+        def load_next():
+            if state["loaded"] < len(loads):
+                kind, n = loads[state["loaded"]]
+                state["loaded"] += 1
+                load(kind, n)
+
+        for i in range(3):
+            load_next()
+        pa_full = const.tile([P, V * V], BF16)
+        nc.sync.dma_start(
+            out=pa_full[:],
+            in_=PA.rearrange("s v w -> s (v w)").unsqueeze(1).to_broadcast([S, 8, V * V]),
+        )
+        for i in range(RAW_BUFS - 3):
+            load_next()
+
+        def regroup(dst, src, n, engine):
+            if engine == "v":
+                if n == 1:
+                    nc.vector.tensor_copy(
+                        out=dst.rearrange("p (c i t) -> p c t i", i=4, t=4),
+                        in_=src.rearrange("p (t c i) -> p c t i", t=4, i=4),
+                    )
+                else:
+                    nc.vector.tensor_copy(
+                        out=dst.rearrange("p (n c i t) -> p n c t i", n=n, i=4, t=4),
+                        in_=src.rearrange("p (n t c i) -> p n c t i", n=n, t=4, i=4),
+                    )
+            else:
+                w = 2048 // n
+                for b in range(n):
+                    nc.scalar.copy(
+                        out=dst[:, w * b : w * b + w].rearrange("p (c i t) -> p c t i", i=4, t=4),
+                        in_=src[:, w * b : w * b + w].rearrange("p (t c i) -> p c t i", t=4, i=4),
+                    )
+
+        def quantise(codes, scales, c0, width, src):
+            nc.vector.quantize_mx(
+                out=codes[:, c0 : c0 + width].bitcast(FP8X4), scales=scales[:, c0 : c0 + width], in_=src
+            )
+
+        m8 = const.tile([P, 8], F32)
+        nc.vector.tensor_reduce(
+            out=m8[:], in_=ident32[:].rearrange("p (s w) -> p w s", w=8), axis=AX.X, op=ALU.add
+        )
+        m4 = const.tile([P, 4], F32)
+        nc.vector.tensor_reduce(
+            out=m4[:], in_=ident32[:].rearrange("p (o v) -> p o v", o=4), axis=AX.X, op=ALU.add
+        )
+
+        grp_a0 = grp_pool.tile([P, 2048], BF16, tag="grp", name="grp_a0", align_bytes=64)
+        regroup(grp_a0[:], raws[("a", 0)][:], 1, "v")
+        load_next()
+
+        quantise(a_codes, a_scales, 0, 512, grp_a0[:])
+
+        def w_transposes(c):
+            r32 = raws[("w", c)][:].bitcast(F32)
+            g = grp_pool.tile([P, 2048], BF16, tag="grp", name="grp_w", align_bytes=64)
+            g32 = g[:].bitcast(F32)
+            banks = []
+            for a in range(2):
+                wt = ps_t.tile([P, 512], F32, tag="tp", name="wt")
+                banks.append(wt)
+                for b in range(2):
+                    for u in range(2):
+                        col = (2 * a + b) * 256
+                        nc.tensor.transpose(
+                            wt[:, (2 * b + u) * 128 : (2 * b + u) * 128 + 128],
+                            r32[:, col + u : col + 256 : 2],
+                            ident32[:],
+                        )
+            for a in range(2):
+                dst = g32[:, 512 * a : 512 * a + 512].rearrange("q (b o u) -> q b o u", b=2, u=2)
+                src = banks[a][:].rearrange("q (b u o) -> q b o u", b=2, u=2)
+                if a == 0:
+                    nc.scalar.copy(out=dst, in_=src)
+                else:
+                    nc.vector.tensor_copy(out=dst, in_=src)
+            load_next()
+            return g
+
+        grouped = {}
+
+        def quantise_oldest():
+            g = state["quantised"]
+            state["quantised"] = g + 1
+            quantise(f_codes, f_scales, 512 * g, 512, grouped[g][:])
+
+        def feat_step(engine):
+            g = state["next"]
+            state["next"] = g + 1
+            gt = grp_pool.tile([P, 2048], BF16, tag="grp", name="grp_f", align_bytes=64)
+            regroup(gt[:], raws[("f", g)][:], 4, engine)
+            load_next()
+            grouped[g] = gt
+            while state["quantised"] < g:
+                quantise_oldest()
+
+        def first_pass(h, s):
+            acc = ps_m.tile([P, 512], F32, tag="mm", name="acc")
+            nc.tensor.matmul_mx(
+                out=acc[:],
+                lhsT=w_codes[:, P * s : P * s + P].bitcast(FP8X4),
+                lhsT_scale=w_scales[:, P * s : P * s + P],
+                rhs=a_codes[:, 512 * h : 512 * h + 512].bitcast(FP8X4),
+                rhs_scale=a_scales[:, 512 * h : 512 * h + 512],
+                start=True,
+                stop=True,
+            )
+            return acc
+
+        def add_bias(xh, s, acc):
+            nc.scalar.activation(
+                out=xh[:].rearrange("o (v j s w) -> o v j s w", v=16, j=4, s=S)[:, :, :, s, :],
+                in_=acc[:].rearrange("o (v w j) -> o v j w", v=16, j=4),
+                func=ACT.Identity,
+                bias=cst[:, 4 + s : 5 + s],
+                scale=1.0,
+            )
+
+        in2 = big.tile([P, COUT * V * 4], BF16, tag="in2", name="in2", align_bytes=64)
+        in2_v = in2[:].rearrange("p (g v o j) -> p g v o j", g=32, v=V, o=4)
+        pa_t = const.tile([P, V * 4], F32)
+
+        def transposes_and_pa(h, xh, n_tiles):
+            for vl in range(16):
+                v = 16 * h + vl
+                tp = ps_t.tile([P, 512], F32, tag="tp", name="tp")
+                for j in range(4):
+                    col = (4 * vl + j) * P
+                    nc.tensor.transpose(tp[:, P * j : P * j + P], xh[:, col : col + P], ident32[:])
+                nc.vector.tensor_tensor(
+                    out=in2_v[:, :, v, :, :],
+                    in0=tp[:].rearrange("p (j g o) -> p g o j", j=4, o=4),
+                    in1=pa_t[:, 4 * v : 4 * v + 4].unsqueeze(1).unsqueeze(1).to_broadcast([P, 32, 4, 4]),
+                    op=ALU.mult,
+                )
+                if evenly(vl, n_tiles, 16):
+                    feat_step("s")
+
+        x0 = big.tile([P, 8192], F32, tag="x", name="x0")
+        grp_w = w_transposes(0)
+        quantise(w_codes, w_scales, 0, 512, grp_w[:])
+        zt = ps_t.tile([P, P], BF16, tag="tp", name="zt")
+        nc.tensor.transpose(zt[:], zrows[:], identb[:])
+        cst = const.tile([P, 20], F32)
+        nc.vector.tensor_copy(out=cst[:], in_=zt[:, 0:20])
+        bn = const.tile([P, 8], F32)
+        nc.vector.tensor_scalar_add(out=bn[:, 0:1], in0=cst[:, 3:4], scalar1=EPS)
+        rep = const.tile([P, 2 * P], F32)
+        scsh = const.tile([P, 64], F32)
+        for c in range(4):
+            if c < 3:
+                grp_w = w_transposes(c + 1)
+            if c == 2:
+                rt = ps_t.tile([P, 2 * P], F32, tag="tp", name="rt")
+                nc.tensor.transpose(rt[:, 0:P], rep[:, 0:P], ident32[:])
+                nc.tensor.transpose(rt[:, P : 2 * P], rep[:, P : 2 * P], ident32[:])
+            accs = [first_pass(0, s) for s in range(4 * c, 4 * c + 4)]
+            if c == 1:
+                nc.vector.reciprocal(out=bn[:, 1:2], in_=sq[:, 1:2])
+                nc.vector.tensor_tensor(out=bn[:, 2:3], in0=cst[:, 0:1], in1=bn[:, 1:2], op=ALU.mult)
+                nc.vector.tensor_tensor(out=bn[:, 3:4], in0=cst[:, 2:3], in1=bn[:, 2:3], op=ALU.mult)
+                nc.vector.tensor_tensor(out=bn[:, 4:5], in0=cst[:, 1:2], in1=bn[:, 3:4], op=ALU.subtract)
+                nc.vector.tensor_copy(out=rep[:, 0:P], in_=bn[:, 2:3].to_broadcast([P, P]))
+                nc.vector.tensor_copy(out=rep[:, P : 2 * P], in_=bn[:, 4:5].to_broadcast([P, P]))
+            if c == 3:
+                bn_sel = const.tile([P, 2 * P], F32)
+                nc.vector.tensor_tensor(
+                    out=bn_sel[:].rearrange("p (c o) -> p c o", o=4),
+                    in0=rt[:].rearrange("p (c o) -> p c o", o=4),
+                    in1=m4[:].unsqueeze(1).to_broadcast([P, 64, 4]),
+                    op=ALU.mult,
+                )
+                nc.vector.tensor_reduce(
+                    out=scsh[:], in_=bn_sel[:].rearrange("p (c o) -> p c o", o=4), axis=AX.X, op=ALU.add
+                )
+            if c == 0:
+                pa_sel = const.tile([P, V * V], F32)
+                nc.vector.tensor_tensor(
+                    out=pa_sel[:].rearrange("p (v j w) -> p v j w", v=V, j=4),
+                    in0=pa_full[:].rearrange("p (v w j) -> p v j w", v=V, j=4),
+                    in1=m8[:].unsqueeze(1).unsqueeze(1).to_broadcast([P, V, 4, 8]),
+                    op=ALU.mult,
+                )
+                nc.vector.tensor_reduce(
+                    out=pa_t[:], in_=pa_sel[:].rearrange("p (c w) -> p c w", w=8), axis=AX.X, op=ALU.add
+                )
+            if c < 3:
+                quantise(w_codes, w_scales, 512 * (c + 1), 512, grp_w[:])
+            for s in range(4 * c, 4 * c + 4):
+                add_bias(x0, s, accs[s - 4 * c])
+            if c == 0:
+                nc.scalar.sqrt(out=sq[:, 1:2], in_=bn[:, 0:1])
+            if c == 3:
+                grp_a1 = grp_pool.tile([P, 2048], BF16, tag="grp", name="grp_a1", align_bytes=64)
+                regroup(grp_a1[:], raws[("a", 1)][:], 1, "v")
+                load_next()
+            if c > 0:
+                feat_step("v")
+        quantise(a_codes, a_scales, 512, 512, grp_a1[:])
+        transposes_and_pa(0, x0, TILES_T0)
+        x1 = big.tile([P, 8192], F32, tag="x", name="x1")
+        for s in range(S):
+            add_bias(x1, s, first_pass(1, s))
+            if evenly(s, TILES_S1, S):
+                feat_step("v")
+        transposes_and_pa(1, x1, TILES_T1)
+        for c in range(4):
+            quantise(g_codes, g_scales, 1024 * c, 1024, in2[:, 4096 * c : 4096 * c + 4096])
+            if evenly(c, TILES_QG, 4):
+                feat_step("s")
+
+        res_v = res.rearrange("n o v t -> (n o v) t").rearrange("(g p) t -> p g t", p=P)
+        out_v = out.rearrange("n o v t -> (n o v) t").rearrange("(g p) t -> p g t", p=P)
+        late = big.tile([P, 8192], F32, tag="x", name="late")
+        res_tiles = {}
+
+        def load_res(qd):
+            if qd < 8:
+                r = res_pool.tile([P, 4 * T], BF16, tag="res", name="res_t")
+                nc.sync.dma_start(
+                    out=r[:].rearrange("p (g t) -> p g t", g=4), in_=res_v[:, 4 * qd : 4 * qd + 4, :]
+                )
+                res_tiles[qd] = r
+
+        def part(kind, qd):
+            c0 = 2048 * kind + 512 * (qd % 3)
+            return late[:, c0 : c0 + 512]
+
+        def second_passes(qd):
+            while state["quantised"] < 4 * qd + 4:
+                quantise_oldest()
+            banks = [ps_m.tile([P, 512], F32, tag="mm", name="s2") for o in range(4)]
+            for k in range(4):
+                g = 4 * qd + k
+                for o in range(4):
+                    ch = 4 * g + o
+                    nc.tensor.matmul_mx(
+                        out=banks[o][:, P * k : P * k + P],
+                        lhsT=f_codes[:, P * ch : P * ch + P].bitcast(FP8X4),
+                        lhsT_scale=f_scales[:, P * ch : P * ch + P],
+                        rhs=g_codes[:, P * g : P * g + P].bitcast(FP8X4),
+                        rhs_scale=g_scales[:, P * g : P * g + P],
+                        start=True,
+                        stop=True,
+                    )
+            for o in range(4):
+                nc.scalar.copy(
+                    out=part(0, qd).rearrange("t (k o v) -> t k o v", k=4, o=4)[:, :, o, :],
+                    in_=banks[o][:].rearrange("t (k v o) -> t k v o", k=4, o=4)[:, :, :, o],
+                )
+
+        def back_and_norm(qd):
+            ft = ps_t.tile([P, 512], F32, tag="tp", name="ft")
+            for k in range(4):
+                nc.tensor.transpose(
+                    ft[:, P * k : P * k + P], part(0, qd)[:, P * k : P * k + P], ident32[:]
+                )
+            for k in range(4):
+                g = 4 * qd + k
+                nc.vector.scalar_tensor_tensor(
+                    out=part(1, qd)[:, P * k : P * k + P],
+                    in0=ft[:, P * k : P * k + P],
+                    scalar=scsh[:, g : g + 1],
+                    in1=res_tiles[qd][:, T * k : T * k + T],
+                    op0=ALU.mult,
+                    op1=ALU.add,
+                )
+
+        def relu_and_store(qd):
+            for k in range(4):
+                g = 4 * qd + k
+                nc.scalar.activation(
+                    out=part(2, qd)[:, P * k : P * k + P],
+                    in_=part(1, qd)[:, P * k : P * k + P],
+                    func=ACT.Relu,
+                    bias=scsh[:, 32 + g : 33 + g],
+                    scale=1.0,
+                )
+            nc.sync.dma_start(
+                out=out_v[:, 4 * qd : 4 * qd + 4, :],
+                in_=part(2, qd).rearrange("p (k t) -> p k t", k=4),
+            )
+
+        load_res(0)
+        load_res(1)
+        first_left = state["next"]
+        left = N_TILES - first_left
+        for i in range(10):
+            if i < 8:
+                want = max(4 * i + 4, first_left + ((i + 1) * left + 7) // 8)
+                while state["next"] < want:
+                    feat_step("s" if (state["next"] - first_left) % 2 == 1 else "v")
+                load_res(i + 2)
+                second_passes(i)
+            if 1 <= i <= 8:
+                back_and_norm(i - 1)
+            if i >= 2:
+                relu_and_store(i - 2)

@@ -17,12 +17,21 @@ S, CIN, COUT, V, T = 16, 512, 128, 32, 128
 EPS = 1e-5
 FLOPS = 2 * S * COUT * CIN * V * V + 2 * COUT * V * S * V * T
 N_TILES = COUT // 4
-RAW_BUFS = 6
-TILES_T0, TILES_S1, TILES_T1, TILES_QG = 7, 6, 5, 2
+RAW_BUFS = 5
+PLAN_W = "vvv"
+PLAN_T0 = {"s": 4, "g": 3, "t": 2}
+PLAN_S1 = {"v": 3, "s": 1}
+PLAN_T1 = {"s": 3, "g": 3, "t": 2}
+PLAN_QG = {"s": 2}
+PLAN_END = "svvsss"
 
 
 def evenly(i, n, total):
     return (i + 1) * n // total > i * n // total
+
+
+def spread(counts, total):
+    return ["".join(e for e in counts if evenly(i, counts[e], total)) for i in range(total)]
 
 
 def tile_multiscale_gcn_pa_kernel(
@@ -35,9 +44,9 @@ def tile_multiscale_gcn_pa_kernel(
         big = ctx.enter_context(tc.tile_pool(name="big", bufs=1))
         raw_pool = ctx.enter_context(tc.tile_pool(name="rawp", bufs=RAW_BUFS))
         grp_pool = ctx.enter_context(tc.tile_pool(name="grpp", bufs=4))
-        res_pool = ctx.enter_context(tc.tile_pool(name="resp", bufs=4))
-        ps_m = ctx.enter_context(tc.psum_pool(name="psm", bufs=4))
-        ps_t = ctx.enter_context(tc.psum_pool(name="pst", bufs=4))
+        slow_pool = ctx.enter_context(tc.tile_pool(name="slowp", bufs=2))
+        res_pool = ctx.enter_context(tc.tile_pool(name="resp", bufs=3))
+        ps = ctx.enter_context(tc.psum_pool(name="ps", bufs=8))
         ctx.enter_context(tc.manual_schedule())
 
         w_codes = keep.tile([P, S * COUT], U32, align_bytes=64)
@@ -49,31 +58,43 @@ def tile_multiscale_gcn_pa_kernel(
         f_codes = keep.tile([P, COUT * T], U32, align_bytes=64)
         f_scales = keep.tile([P, COUT * T], U8, align_bytes=64)
 
-        zrows = const.tile([P, P], BF16)
-        nc.vector.memset(zrows[:], 0.0)
+        plan_t0 = spread(PLAN_T0, 16)
+        plan_s1 = spread(PLAN_S1, 16)
+        plan_t1 = spread(PLAN_T1, 16)
+        plan_qg = spread(PLAN_QG, 4)
+        order = PLAN_W + "".join(plan_t0 + plan_s1 + plan_t1 + plan_qg) + PLAN_END
+        assert len(order) == N_TILES
+
         sq = const.tile([P, 2], F32)
         nc.vector.memset(sq[:], 1.0)
         nc.scalar.sqrt(out=sq[:, 1:2], in_=sq[:, 0:1])
+        b_rows = const.tile([P, P], BF16)
+        nc.vector.memset(b_rows[:], 0.0)
+        pa_rows = const.tile([P, S * V], BF16)
+        nc.vector.memset(pa_rows[:], 0.0)
+        bn_rows = const.tile([P, P], BF16)
+        nc.vector.memset(bn_rows[:], 0.0)
         ident32 = const.tile([P, P], F32)
         make_identity(nc, ident32[:])
         identb = const.tile([P, P], BF16)
         make_identity(nc, identb[:])
-        nc.scalar.dma_start(out=zrows[4:20, :], in_=ada_b)
-        nc.scalar.dma_start(out=zrows[3:4, :], in_=bn_var.unsqueeze(0))
-        nc.scalar.dma_start(out=zrows[0:1, :], in_=bn_gamma.unsqueeze(0))
-        nc.scalar.dma_start(out=zrows[1:2, :], in_=bn_beta.unsqueeze(0))
-        nc.scalar.dma_start(out=zrows[2:3, :], in_=bn_mean.unsqueeze(0))
-
+        nc.scalar.dma_start(out=b_rows[0:S, :], in_=ada_b)
+        nc.scalar.dma_start(
+            out=pa_rows[0:V, :].rearrange("v (s w) -> v s w", s=S), in_=PA.rearrange("s v w -> v s w")
+        )
         a2 = ada_A.rearrange("n i v w -> (n i) (v w)")
         raws = {}
 
         def load(kind, n):
-            r = raw_pool.tile([P, 2048], BF16, tag="raw", name="raw")
+            if kind == "f" and order[n] == "g":
+                r = slow_pool.tile([P, 2048], BF16, tag="raws", name="raw_s")
+            else:
+                r = raw_pool.tile([P, 2048], BF16, tag="raw", name="raw")
             raws[(kind, n)] = r
             if kind == "a":
-                r3 = r[:].rearrange("q (t c) -> q t c", t=4)
                 nc.sync.dma_start(
-                    out=r3, in_=a2[:, 512 * n : 512 * n + 512].rearrange("(q t) c -> q t c", t=4)
+                    out=r[:].rearrange("q (t c) -> q t c", t=4),
+                    in_=a2[:, 512 * n : 512 * n + 512].rearrange("(q t) c -> q t c", t=4),
                 )
             elif kind == "w":
                 nc.sync.dma_start(
@@ -89,7 +110,7 @@ def tile_multiscale_gcn_pa_kernel(
 
         loads = [("a", 0), ("w", 0), ("w", 1), ("w", 2), ("f", 0), ("w", 3), ("f", 1), ("a", 1)]
         loads.extend([("f", g) for g in range(2, N_TILES)])
-        state = {"loaded": 0, "next": 0, "quantised": 0}
+        state = {"loaded": 0, "next": 0}
 
         def load_next():
             if state["loaded"] < len(loads):
@@ -97,34 +118,39 @@ def tile_multiscale_gcn_pa_kernel(
                 state["loaded"] += 1
                 load(kind, n)
 
-        for i in range(3):
-            load_next()
-        pa_full = const.tile([P, V * V], BF16)
-        nc.sync.dma_start(
-            out=pa_full[:],
-            in_=PA.rearrange("s v w -> s (v w)").unsqueeze(1).to_broadcast([S, 8, V * V]),
-        )
-        for i in range(RAW_BUFS - 3):
+        for i in range(RAW_BUFS):
             load_next()
 
+        for row, vec in enumerate((bn_gamma, bn_beta, bn_mean, bn_var)):
+            nc.scalar.dma_start(out=bn_rows[row : row + 1, :], in_=vec.unsqueeze(0))
+        m16 = const.tile([P, 16], F32)
+        nc.vector.tensor_reduce(
+            out=m16[:], in_=ident32[:].rearrange("p (o v) -> p o v", o=16), axis=AX.X, op=ALU.add
+        )
+
         def regroup(dst, src, n, engine):
+            w = 2048 // n
             if engine == "v":
-                if n == 1:
-                    nc.vector.tensor_copy(
-                        out=dst.rearrange("p (c i t) -> p c t i", i=4, t=4),
-                        in_=src.rearrange("p (t c i) -> p c t i", t=4, i=4),
+                nc.vector.tensor_copy(
+                    out=dst.rearrange("p (n c i t) -> p n c t i", n=n, i=4, t=4),
+                    in_=src.rearrange("p (n t c i) -> p n c t i", n=n, t=4, i=4),
+                )
+                return
+            for b in range(n):
+                d, r = dst[:, w * b : w * b + w], src[:, w * b : w * b + w]
+                if engine == "s":
+                    nc.scalar.copy(
+                        out=d.rearrange("p (c i t) -> p c t i", i=4, t=4),
+                        in_=r.rearrange("p (t c i) -> p c t i", t=4, i=4),
                     )
                 else:
-                    nc.vector.tensor_copy(
-                        out=dst.rearrange("p (n c i t) -> p n c t i", n=n, i=4, t=4),
-                        in_=src.rearrange("p (n t c i) -> p n c t i", n=n, t=4, i=4),
-                    )
-            else:
-                w = 2048 // n
-                for b in range(n):
-                    nc.scalar.copy(
-                        out=dst[:, w * b : w * b + w].rearrange("p (c i t) -> p c t i", i=4, t=4),
-                        in_=src[:, w * b : w * b + w].rearrange("p (t c i) -> p c t i", t=4, i=4),
+                    nc.gpsimd.tensor_scalar(
+                        out=d.rearrange("p (c t) -> p c t", t=4),
+                        in0=r.rearrange("p (t c) -> p c t", t=4),
+                        scalar1=1.0,
+                        scalar2=0.0,
+                        op0=ALU.mult,
+                        op1=ALU.add,
                     )
 
         def quantise(codes, scales, c0, width, src):
@@ -132,19 +158,27 @@ def tile_multiscale_gcn_pa_kernel(
                 out=codes[:, c0 : c0 + width].bitcast(FP8X4), scales=scales[:, c0 : c0 + width], in_=src
             )
 
-        m8 = const.tile([P, 8], F32)
-        nc.vector.tensor_reduce(
-            out=m8[:], in_=ident32[:].rearrange("p (s w) -> p w s", w=8), axis=AX.X, op=ALU.add
-        )
-        m4 = const.tile([P, 4], F32)
-        nc.vector.tensor_reduce(
-            out=m4[:], in_=ident32[:].rearrange("p (o v) -> p o v", o=4), axis=AX.X, op=ALU.add
-        )
+        def regroup_a(n, engine):
+            g = grp_pool.tile([P, 2048], BF16, tag="grp", name="grp_a", align_bytes=64)
+            if engine == "v":
+                nc.vector.tensor_copy(
+                    out=g[:].rearrange("p (c i t) -> p c t i", i=4, t=4),
+                    in_=raws[("a", n)][:].rearrange("p (t c i) -> p c t i", t=4, i=4),
+                )
+            else:
+                for b in range(4):
+                    nc.gpsimd.tensor_scalar(
+                        out=g[:, 512 * b : 512 * b + 512].rearrange("p (c t) -> p c t", t=4),
+                        in0=raws[("a", n)][:].rearrange("p (t b c) -> p b c t", t=4, b=4)[:, b],
+                        scalar1=1.0,
+                        scalar2=0.0,
+                        op0=ALU.mult,
+                        op1=ALU.add,
+                    )
+            load_next()
+            return g
 
-        grp_a0 = grp_pool.tile([P, 2048], BF16, tag="grp", name="grp_a0", align_bytes=64)
-        regroup(grp_a0[:], raws[("a", 0)][:], 1, "v")
-        load_next()
-
+        grp_a0 = regroup_a(0, "v")
         quantise(a_codes, a_scales, 0, 512, grp_a0[:])
 
         def w_transposes(c):
@@ -153,7 +187,7 @@ def tile_multiscale_gcn_pa_kernel(
             g32 = g[:].bitcast(F32)
             banks = []
             for a in range(2):
-                wt = ps_t.tile([P, 512], F32, tag="tp", name="wt")
+                wt = ps.tile([P, 512], F32, tag="bank", name="wt")
                 banks.append(wt)
                 for b in range(2):
                     for u in range(2):
@@ -174,24 +208,73 @@ def tile_multiscale_gcn_pa_kernel(
             return g
 
         grouped = {}
+        waiting = []
+        slow = []
+        in_banks = []
+        done = set()
 
-        def quantise_oldest():
-            g = state["quantised"]
-            state["quantised"] = g + 1
-            quantise(f_codes, f_scales, 512 * g, 512, grouped[g][:])
+        def quantise_tile(g):
+            if g not in done:
+                done.add(g)
+                quantise(f_codes, f_scales, 512 * g, 512, grouped[g][:])
+
+        def quantise_waiting():
+            for g in list(waiting):
+                quantise_tile(g)
+            waiting.clear()
+
+        def quantise_slow():
+            if len(slow) > 0:
+                quantise_tile(slow.pop(0))
 
         def feat_step(engine):
             g = state["next"]
+            assert order[g] == engine
             state["next"] = g + 1
-            gt = grp_pool.tile([P, 2048], BF16, tag="grp", name="grp_f", align_bytes=64)
-            regroup(gt[:], raws[("f", g)][:], 4, engine)
-            load_next()
+            src = raws[("f", g)][:]
+            if engine == "t":
+                banks = []
+                for half in range(2):
+                    bank = ps.tile([P, 1024], BF16, tag="bank", name="bank")
+                    banks.append(bank)
+                    for c in range(2):
+                        col = 1024 * half + 512 * c
+                        nc.tensor.matmul(
+                            out=bank[:, 512 * c : 512 * c + 512].rearrange("p (c t) -> p c t", t=4),
+                            lhsT=identb[:],
+                            rhs=src[:, col : col + 512].rearrange("p (t c) -> p c t", t=4),
+                            start=True,
+                            stop=True,
+                        )
+                in_banks.append((g, banks))
+                load_next()
+                return
+            if engine == "g":
+                gt = slow_pool.tile([P, 2048], BF16, tag="grps", name="grp_s", align_bytes=64)
+            else:
+                gt = grp_pool.tile([P, 2048], BF16, tag="grp", name="grp_f", align_bytes=64)
             grouped[g] = gt
-            while state["quantised"] < g:
-                quantise_oldest()
+            regroup(gt[:], src, 4, engine)
+            load_next()
+            if engine == "g":
+                slow.append(g)
+            else:
+                quantise_waiting()
+                waiting.append(g)
+
+        def feat_out_of_banks():
+            if len(in_banks) == 0:
+                return
+            g, banks = in_banks.pop(0)
+            gt = grp_pool.tile([P, 2048], BF16, tag="grp", name="grp_f", align_bytes=64)
+            grouped[g] = gt
+            for half in range(2):
+                nc.scalar.copy(out=gt[:, 1024 * half : 1024 * half + 1024], in_=banks[half][:])
+            quantise_waiting()
+            waiting.append(g)
 
         def first_pass(h, s):
-            acc = ps_m.tile([P, 512], F32, tag="mm", name="acc")
+            acc = ps.tile([P, 512], F32, tag="bank", name="acc")
             nc.tensor.matmul_mx(
                 out=acc[:],
                 lhsT=w_codes[:, P * s : P * s + P].bitcast(FP8X4),
@@ -208,7 +291,7 @@ def tile_multiscale_gcn_pa_kernel(
                 out=xh[:].rearrange("o (v j s w) -> o v j s w", v=16, j=4, s=S)[:, :, :, s, :],
                 in_=acc[:].rearrange("o (v w j) -> o v j w", v=16, j=4),
                 func=ACT.Identity,
-                bias=cst[:, 4 + s : 5 + s],
+                bias=bias[:, s : s + 1],
                 scale=1.0,
             )
 
@@ -216,10 +299,10 @@ def tile_multiscale_gcn_pa_kernel(
         in2_v = in2[:].rearrange("p (g v o j) -> p g v o j", g=32, v=V, o=4)
         pa_t = const.tile([P, V * 4], F32)
 
-        def transposes_and_pa(h, xh, n_tiles):
+        def transposes_and_pa(h, xh, plan):
             for vl in range(16):
                 v = 16 * h + vl
-                tp = ps_t.tile([P, 512], F32, tag="tp", name="tp")
+                tp = ps.tile([P, 512], F32, tag="bank", name="tp")
                 for j in range(4):
                     col = (4 * vl + j) * P
                     nc.tensor.transpose(tp[:, P * j : P * j + P], xh[:, col : col + P], ident32[:])
@@ -229,29 +312,42 @@ def tile_multiscale_gcn_pa_kernel(
                     in1=pa_t[:, 4 * v : 4 * v + 4].unsqueeze(1).unsqueeze(1).to_broadcast([P, 32, 4, 4]),
                     op=ALU.mult,
                 )
-                if evenly(vl, n_tiles, 16):
-                    feat_step("s")
+                if vl % 4 == 3:
+                    feat_out_of_banks()
+                for e in plan[vl]:
+                    feat_step(e)
+                if len(slow) > 1:
+                    quantise_slow()
 
         x0 = big.tile([P, 8192], F32, tag="x", name="x0")
         grp_w = w_transposes(0)
         quantise(w_codes, w_scales, 0, 512, grp_w[:])
-        zt = ps_t.tile([P, P], BF16, tag="tp", name="zt")
-        nc.tensor.transpose(zt[:], zrows[:], identb[:])
-        cst = const.tile([P, 20], F32)
-        nc.vector.tensor_copy(out=cst[:], in_=zt[:, 0:20])
+        bt = ps.tile([P, P], BF16, tag="bank", name="bt")
+        nc.tensor.transpose(bt[:], b_rows[:], identb[:])
+        bias = const.tile([P, S], F32)
+        nc.vector.tensor_copy(out=bias[:], in_=bt[:, 0:S])
+        cst = const.tile([P, 4], F32)
         bn = const.tile([P, 8], F32)
-        nc.vector.tensor_scalar_add(out=bn[:, 0:1], in0=cst[:, 3:4], scalar1=EPS)
         rep = const.tile([P, 2 * P], F32)
-        scsh = const.tile([P, 64], F32)
+        scsh = const.tile([P, 16], F32)
         for c in range(4):
             if c < 3:
                 grp_w = w_transposes(c + 1)
-            if c == 2:
-                rt = ps_t.tile([P, 2 * P], F32, tag="tp", name="rt")
+            if c == 0:
+                pt = ps.tile([P, 4 * P], BF16, tag="bank", name="pt")
+                for j in range(4):
+                    nc.tensor.transpose(pt[:, P * j : P * j + P], pa_rows[:, j : 512 : 4], identb[:])
+            if c == 1:
+                zt = ps.tile([P, P], BF16, tag="bank", name="zt")
+                nc.tensor.transpose(zt[:], bn_rows[:], identb[:])
+                nc.vector.tensor_copy(out=cst[:], in_=zt[:, 0:4])
+                nc.vector.tensor_scalar_add(out=bn[:, 0:1], in0=cst[:, 3:4], scalar1=EPS)
+            if c == 3:
+                rt = ps.tile([P, 2 * P], F32, tag="bank", name="rt")
                 nc.tensor.transpose(rt[:, 0:P], rep[:, 0:P], ident32[:])
                 nc.tensor.transpose(rt[:, P : 2 * P], rep[:, P : 2 * P], ident32[:])
             accs = [first_pass(0, s) for s in range(4 * c, 4 * c + 4)]
-            if c == 1:
+            if c == 2:
                 nc.vector.reciprocal(out=bn[:, 1:2], in_=sq[:, 1:2])
                 nc.vector.tensor_tensor(out=bn[:, 2:3], in0=cst[:, 0:1], in1=bn[:, 1:2], op=ALU.mult)
                 nc.vector.tensor_tensor(out=bn[:, 3:4], in0=cst[:, 2:3], in1=bn[:, 2:3], op=ALU.mult)
@@ -261,61 +357,56 @@ def tile_multiscale_gcn_pa_kernel(
             if c == 3:
                 bn_sel = const.tile([P, 2 * P], F32)
                 nc.vector.tensor_tensor(
-                    out=bn_sel[:].rearrange("p (c o) -> p c o", o=4),
-                    in0=rt[:].rearrange("p (c o) -> p c o", o=4),
-                    in1=m4[:].unsqueeze(1).to_broadcast([P, 64, 4]),
+                    out=bn_sel[:].rearrange("p (c o) -> p c o", o=16),
+                    in0=rt[:].rearrange("p (c o) -> p c o", o=16),
+                    in1=m16[:].unsqueeze(1).to_broadcast([P, 16, 16]),
                     op=ALU.mult,
                 )
                 nc.vector.tensor_reduce(
-                    out=scsh[:], in_=bn_sel[:].rearrange("p (c o) -> p c o", o=4), axis=AX.X, op=ALU.add
+                    out=scsh[:], in_=bn_sel[:].rearrange("p (c o) -> p c o", o=16), axis=AX.X, op=ALU.add
                 )
             if c == 0:
-                pa_sel = const.tile([P, V * V], F32)
-                nc.vector.tensor_tensor(
-                    out=pa_sel[:].rearrange("p (v j w) -> p v j w", v=V, j=4),
-                    in0=pa_full[:].rearrange("p (v w j) -> p v j w", v=V, j=4),
-                    in1=m8[:].unsqueeze(1).unsqueeze(1).to_broadcast([P, V, 4, 8]),
-                    op=ALU.mult,
-                )
-                nc.vector.tensor_reduce(
-                    out=pa_t[:], in_=pa_sel[:].rearrange("p (c w) -> p c w", w=8), axis=AX.X, op=ALU.add
+                nc.vector.tensor_copy(
+                    out=pa_t[:].rearrange("p (v j) -> p v j", j=4),
+                    in_=pt[:].rearrange("p (j v) -> p v j", j=4)[:, 0:V, :],
                 )
             if c < 3:
                 quantise(w_codes, w_scales, 512 * (c + 1), 512, grp_w[:])
             for s in range(4 * c, 4 * c + 4):
                 add_bias(x0, s, accs[s - 4 * c])
-            if c == 0:
+            if c == 1:
                 nc.scalar.sqrt(out=sq[:, 1:2], in_=bn[:, 0:1])
             if c == 3:
-                grp_a1 = grp_pool.tile([P, 2048], BF16, tag="grp", name="grp_a1", align_bytes=64)
-                regroup(grp_a1[:], raws[("a", 1)][:], 1, "v")
-                load_next()
+                grp_a1 = regroup_a(1, "v")
             if c > 0:
-                feat_step("v")
+                for e in PLAN_W[c - 1]:
+                    feat_step(e)
         quantise(a_codes, a_scales, 512, 512, grp_a1[:])
-        transposes_and_pa(0, x0, TILES_T0)
+        transposes_and_pa(0, x0, plan_t0)
+        feat_out_of_banks()
         x1 = big.tile([P, 8192], F32, tag="x", name="x1")
         for s in range(S):
             add_bias(x1, s, first_pass(1, s))
-            if evenly(s, TILES_S1, S):
-                feat_step("v")
-        transposes_and_pa(1, x1, TILES_T1)
+            if s % 5 == 4:
+                quantise_slow()
+            for e in plan_s1[s]:
+                feat_step(e)
+        transposes_and_pa(1, x1, plan_t1)
+        feat_out_of_banks()
         for c in range(4):
             quantise(g_codes, g_scales, 1024 * c, 1024, in2[:, 4096 * c : 4096 * c + 4096])
-            if evenly(c, TILES_QG, 4):
-                feat_step("s")
+            for e in plan_qg[c]:
+                feat_step(e)
 
-        res_v = res.rearrange("n o v t -> (n o v) t").rearrange("(g p) t -> p g t", p=P)
-        out_v = out.rearrange("n o v t -> (n o v) t").rearrange("(g p) t -> p g t", p=P)
+        res_v = res.rearrange("n o v t -> (n o v t)").rearrange("(g p f) -> g p f", p=P, f=512)
+        out_v = out.rearrange("n o v t -> (n o v t)").rearrange("(g p f) -> g p f", p=P, f=512)
         late = big.tile([P, 8192], F32, tag="x", name="late")
         res_tiles = {}
 
         def load_res(qd):
             if qd < 8:
-                r = res_pool.tile([P, 4 * T], BF16, tag="res", name="res_t")
-                nc.sync.dma_start(
-                    out=r[:].rearrange("p (g t) -> p g t", g=4), in_=res_v[:, 4 * qd : 4 * qd + 4, :]
-                )
+                r = res_pool.tile([P, 512], BF16, tag="res", name="res_t")
+                nc.sync.dma_start(out=r[:], in_=res_v[qd])
                 res_tiles[qd] = r
 
         def part(kind, qd):
@@ -323,15 +414,17 @@ def tile_multiscale_gcn_pa_kernel(
             return late[:, c0 : c0 + 512]
 
         def second_passes(qd):
-            while state["quantised"] < 4 * qd + 4:
-                quantise_oldest()
-            banks = [ps_m.tile([P, 512], F32, tag="mm", name="s2") for o in range(4)]
-            for k in range(4):
-                g = 4 * qd + k
-                for o in range(4):
+            for g in range(4 * qd, 4 * qd + 4):
+                quantise_tile(g)
+                if g in waiting:
+                    waiting.remove(g)
+            for o in range(4):
+                bank = ps.tile([P, 512], F32, tag="bank", name="s2")
+                for k in range(4):
+                    g = 4 * qd + k
                     ch = 4 * g + o
                     nc.tensor.matmul_mx(
-                        out=banks[o][:, P * k : P * k + P],
+                        out=bank[:, P * k : P * k + P],
                         lhsT=f_codes[:, P * ch : P * ch + P].bitcast(FP8X4),
                         lhsT_scale=f_scales[:, P * ch : P * ch + P],
                         rhs=g_codes[:, P * g : P * g + P].bitcast(FP8X4),
@@ -339,56 +432,53 @@ def tile_multiscale_gcn_pa_kernel(
                         start=True,
                         stop=True,
                     )
-            for o in range(4):
                 nc.scalar.copy(
-                    out=part(0, qd).rearrange("t (k o v) -> t k o v", k=4, o=4)[:, :, o, :],
-                    in_=banks[o][:].rearrange("t (k v o) -> t k v o", k=4, o=4)[:, :, :, o],
+                    out=part(0, qd).rearrange("t (i k o b) -> t o k i b", i=4, k=4, o=4)[:, o],
+                    in_=bank[:].rearrange("t (k b i o) -> t o k i b", k=4, i=4, o=4)[:, o],
                 )
 
         def back_and_norm(qd):
-            ft = ps_t.tile([P, 512], F32, tag="tp", name="ft")
-            for k in range(4):
+            ft = ps.tile([P, 512], F32, tag="bank", name="ft")
+            for i in range(4):
                 nc.tensor.transpose(
-                    ft[:, P * k : P * k + P], part(0, qd)[:, P * k : P * k + P], ident32[:]
+                    ft[:, P * i : P * i + P], part(0, qd)[:, P * i : P * i + P], ident32[:]
                 )
-            for k in range(4):
-                g = 4 * qd + k
-                nc.vector.scalar_tensor_tensor(
-                    out=part(1, qd)[:, P * k : P * k + P],
-                    in0=ft[:, P * k : P * k + P],
-                    scalar=scsh[:, g : g + 1],
-                    in1=res_tiles[qd][:, T * k : T * k + T],
-                    op0=ALU.mult,
-                    op1=ALU.add,
-                )
+            nc.vector.scalar_tensor_tensor(
+                out=part(1, qd),
+                in0=ft[:],
+                scalar=scsh[:, qd : qd + 1],
+                in1=res_tiles[qd][:],
+                op0=ALU.mult,
+                op1=ALU.add,
+            )
 
         def relu_and_store(qd):
-            for k in range(4):
-                g = 4 * qd + k
-                nc.scalar.activation(
-                    out=part(2, qd)[:, P * k : P * k + P],
-                    in_=part(1, qd)[:, P * k : P * k + P],
-                    func=ACT.Relu,
-                    bias=scsh[:, 32 + g : 33 + g],
-                    scale=1.0,
-                )
-            nc.sync.dma_start(
-                out=out_v[:, 4 * qd : 4 * qd + 4, :],
-                in_=part(2, qd).rearrange("p (k t) -> p k t", k=4),
+            nc.vector.tensor_scalar(
+                out=part(2, qd),
+                in0=part(1, qd),
+                scalar1=scsh[:, 8 + qd : 9 + qd],
+                scalar2=0.0,
+                op0=ALU.add,
+                op1=ALU.max,
             )
+            nc.sync.dma_start(out=out_v[qd], in_=part(2, qd))
 
         load_res(0)
         load_res(1)
         first_left = state["next"]
         left = N_TILES - first_left
+
+        def feats_until(want):
+            while state["next"] < want:
+                feat_step(order[state["next"]])
+
+        feats_until(4)
         for i in range(10):
             if i < 8:
-                want = max(4 * i + 4, first_left + ((i + 1) * left + 7) // 8)
-                while state["next"] < want:
-                    feat_step("s" if (state["next"] - first_left) % 2 == 1 else "v")
-                load_res(i + 2)
                 second_passes(i)
             if 1 <= i <= 8:
                 back_and_norm(i - 1)
             if i >= 2:
                 relu_and_store(i - 2)
+            load_res(i + 2)
+            feats_until(min(N_TILES, max(4 * i + 8, first_left + ((i + 1) * left + 6) // 7)))

@@ -19,11 +19,11 @@ FLOPS = 2 * S * COUT * CIN * V * V + 2 * COUT * V * S * V * T
 N_TILES = COUT // 4
 RAW_BUFS = 5
 PLAN_W = "vvv"
-PLAN_T0 = {"s": 4, "g": 3, "t": 2}
-PLAN_S1 = {"v": 3, "s": 1}
-PLAN_T1 = {"s": 3, "g": 3, "t": 2}
-PLAN_QG = {"s": 2}
-PLAN_END = "svvsss"
+PLAN_T0 = {"s": 5, "g": 2}
+PLAN_S1 = {"v": 5}
+PLAN_T1 = {"s": 5, "g": 2}
+PLAN_QG = {"s": 2, "v": 0}
+PLAN_END = "ssvvsvvs"
 
 
 def evenly(i, n, total):
@@ -316,8 +316,6 @@ def tile_multiscale_gcn_pa_kernel(
                     feat_out_of_banks()
                 for e in plan[vl]:
                     feat_step(e)
-                if len(slow) > 1:
-                    quantise_slow()
 
         x0 = big.tile([P, 8192], F32, tag="x", name="x0")
         grp_w = w_transposes(0)
@@ -395,6 +393,7 @@ def tile_multiscale_gcn_pa_kernel(
         feat_out_of_banks()
         for c in range(4):
             quantise(g_codes, g_scales, 1024 * c, 1024, in2[:, 4096 * c : 4096 * c + 4096])
+            quantise_slow()
             for e in plan_qg[c]:
                 feat_step(e)
 

@@ -17,13 +17,16 @@ S, CIN, COUT, V, T = 16, 512, 128, 32, 128
 EPS = 1e-5
 FLOPS = 2 * S * COUT * CIN * V * V + 2 * COUT * V * S * V * T
 N_TILES = COUT // 4
-RAW_BUFS = 5
+RAW_BUFS = 7
 PLAN_W = "vvv"
-PLAN_T0 = {"s": 5, "g": 2}
-PLAN_S1 = {"v": 5}
-PLAN_T1 = {"s": 5, "g": 2}
-PLAN_QG = {"s": 2, "v": 0}
-PLAN_END = "ssvvsvvs"
+PLAN_T0 = {"s": 5}
+PLAN_S1 = {"v": 5, "t": 2}
+PLAN_T1 = {"s": 5, "v": 1}
+PLAN_QG = {"s": 2, "t": 2}
+PLAN_END = "vsvsvss"
+Y_ON_V = (0, 0, 0, 0, 0, 0, 0, 2)
+SPAN = 6
+LAG = 1
 
 
 def evenly(i, n, total):
@@ -312,8 +315,7 @@ def tile_multiscale_gcn_pa_kernel(
                     in1=pa_t[:, 4 * v : 4 * v + 4].unsqueeze(1).unsqueeze(1).to_broadcast([P, 32, 4, 4]),
                     op=ALU.mult,
                 )
-                if vl % 4 == 3:
-                    feat_out_of_banks()
+                feat_out_of_banks()
                 for e in plan[vl]:
                     feat_step(e)
 
@@ -328,6 +330,7 @@ def tile_multiscale_gcn_pa_kernel(
         bn = const.tile([P, 8], F32)
         rep = const.tile([P, 2 * P], F32)
         scsh = const.tile([P, 16], F32)
+        bn_sel = const.tile([P, 2 * P], F32)
         for c in range(4):
             if c < 3:
                 grp_w = w_transposes(c + 1)
@@ -335,34 +338,7 @@ def tile_multiscale_gcn_pa_kernel(
                 pt = ps.tile([P, 4 * P], BF16, tag="bank", name="pt")
                 for j in range(4):
                     nc.tensor.transpose(pt[:, P * j : P * j + P], pa_rows[:, j : 512 : 4], identb[:])
-            if c == 1:
-                zt = ps.tile([P, P], BF16, tag="bank", name="zt")
-                nc.tensor.transpose(zt[:], bn_rows[:], identb[:])
-                nc.vector.tensor_copy(out=cst[:], in_=zt[:, 0:4])
-                nc.vector.tensor_scalar_add(out=bn[:, 0:1], in0=cst[:, 3:4], scalar1=EPS)
-            if c == 3:
-                rt = ps.tile([P, 2 * P], F32, tag="bank", name="rt")
-                nc.tensor.transpose(rt[:, 0:P], rep[:, 0:P], ident32[:])
-                nc.tensor.transpose(rt[:, P : 2 * P], rep[:, P : 2 * P], ident32[:])
             accs = [first_pass(0, s) for s in range(4 * c, 4 * c + 4)]
-            if c == 2:
-                nc.vector.reciprocal(out=bn[:, 1:2], in_=sq[:, 1:2])
-                nc.vector.tensor_tensor(out=bn[:, 2:3], in0=cst[:, 0:1], in1=bn[:, 1:2], op=ALU.mult)
-                nc.vector.tensor_tensor(out=bn[:, 3:4], in0=cst[:, 2:3], in1=bn[:, 2:3], op=ALU.mult)
-                nc.vector.tensor_tensor(out=bn[:, 4:5], in0=cst[:, 1:2], in1=bn[:, 3:4], op=ALU.subtract)
-                nc.vector.tensor_copy(out=rep[:, 0:P], in_=bn[:, 2:3].to_broadcast([P, P]))
-                nc.vector.tensor_copy(out=rep[:, P : 2 * P], in_=bn[:, 4:5].to_broadcast([P, P]))
-            if c == 3:
-                bn_sel = const.tile([P, 2 * P], F32)
-                nc.vector.tensor_tensor(
-                    out=bn_sel[:].rearrange("p (c o) -> p c o", o=16),
-                    in0=rt[:].rearrange("p (c o) -> p c o", o=16),
-                    in1=m16[:].unsqueeze(1).to_broadcast([P, 16, 16]),
-                    op=ALU.mult,
-                )
-                nc.vector.tensor_reduce(
-                    out=scsh[:], in_=bn_sel[:].rearrange("p (c o) -> p c o", o=16), axis=AX.X, op=ALU.add
-                )
             if c == 0:
                 nc.vector.tensor_copy(
                     out=pa_t[:].rearrange("p (v j) -> p v j", j=4),
@@ -372,8 +348,6 @@ def tile_multiscale_gcn_pa_kernel(
                 quantise(w_codes, w_scales, 512 * (c + 1), 512, grp_w[:])
             for s in range(4 * c, 4 * c + 4):
                 add_bias(x0, s, accs[s - 4 * c])
-            if c == 1:
-                nc.scalar.sqrt(out=sq[:, 1:2], in_=bn[:, 0:1])
             if c == 3:
                 grp_a1 = regroup_a(1, "v")
             if c > 0:
@@ -382,20 +356,48 @@ def tile_multiscale_gcn_pa_kernel(
         quantise(a_codes, a_scales, 512, 512, grp_a1[:])
         transposes_and_pa(0, x0, plan_t0)
         feat_out_of_banks()
+        zt = ps.tile([P, P], BF16, tag="bank", name="zt")
+        nc.tensor.transpose(zt[:], bn_rows[:], identb[:])
+        nc.vector.tensor_copy(out=cst[:], in_=zt[:, 0:4])
+        nc.vector.tensor_scalar_add(out=bn[:, 0:1], in0=cst[:, 3:4], scalar1=EPS)
+        nc.scalar.sqrt(out=sq[:, 1:2], in_=bn[:, 0:1])
         x1 = big.tile([P, 8192], F32, tag="x", name="x1")
         for s in range(S):
             add_bias(x1, s, first_pass(1, s))
             if s % 5 == 4:
                 quantise_slow()
+            feat_out_of_banks()
             for e in plan_s1[s]:
                 feat_step(e)
+            if s == 5:
+                nc.vector.reciprocal(out=bn[:, 1:2], in_=sq[:, 1:2])
+                nc.vector.tensor_tensor(out=bn[:, 2:3], in0=cst[:, 0:1], in1=bn[:, 1:2], op=ALU.mult)
+                nc.vector.tensor_tensor(out=bn[:, 3:4], in0=cst[:, 2:3], in1=bn[:, 2:3], op=ALU.mult)
+                nc.vector.tensor_tensor(out=bn[:, 4:5], in0=cst[:, 1:2], in1=bn[:, 3:4], op=ALU.subtract)
+                nc.vector.tensor_copy(out=rep[:, 0:P], in_=bn[:, 2:3].to_broadcast([P, P]))
+                nc.vector.tensor_copy(out=rep[:, P : 2 * P], in_=bn[:, 4:5].to_broadcast([P, P]))
+            if s == 10:
+                rt = ps.tile([P, 2 * P], F32, tag="bank", name="rt")
+                nc.tensor.transpose(rt[:, 0:P], rep[:, 0:P], ident32[:])
+                nc.tensor.transpose(rt[:, P : 2 * P], rep[:, P : 2 * P], ident32[:])
+                nc.vector.tensor_tensor(
+                    out=bn_sel[:].rearrange("p (c o) -> p c o", o=16),
+                    in0=rt[:].rearrange("p (c o) -> p c o", o=16),
+                    in1=m16[:].unsqueeze(1).to_broadcast([P, 16, 16]),
+                    op=ALU.mult,
+                )
+                nc.vector.tensor_reduce(
+                    out=scsh[:], in_=bn_sel[:].rearrange("p (c o) -> p c o", o=16), axis=AX.X, op=ALU.add
+                )
         transposes_and_pa(1, x1, plan_t1)
         feat_out_of_banks()
         for c in range(4):
             quantise(g_codes, g_scales, 1024 * c, 1024, in2[:, 4096 * c : 4096 * c + 4096])
             quantise_slow()
+            feat_out_of_banks()
             for e in plan_qg[c]:
                 feat_step(e)
+        feat_out_of_banks()
 
         res_v = res.rearrange("n o v t -> (n o v t)").rearrange("(g p f) -> g p f", p=P, f=512)
         out_v = out.rearrange("n o v t -> (n o v t)").rearrange("(g p f) -> g p f", p=P, f=512)
@@ -412,29 +414,41 @@ def tile_multiscale_gcn_pa_kernel(
             c0 = 2048 * kind + 512 * (qd % 3)
             return late[:, c0 : c0 + 512]
 
+        def second_pass(ch, bank, k):
+            g = ch // 4
+            nc.tensor.matmul_mx(
+                out=bank[:, P * k : P * k + P],
+                lhsT=f_codes[:, P * ch : P * ch + P].bitcast(FP8X4),
+                lhsT_scale=f_scales[:, P * ch : P * ch + P],
+                rhs=g_codes[:, P * g : P * g + P].bitcast(FP8X4),
+                rhs_scale=g_scales[:, P * g : P * g + P],
+                start=True,
+                stop=True,
+            )
+
         def second_passes(qd):
             for g in range(4 * qd, 4 * qd + 4):
                 quantise_tile(g)
                 if g in waiting:
                     waiting.remove(g)
+            banks = []
             for o in range(4):
                 bank = ps.tile([P, 512], F32, tag="bank", name="s2")
+                banks.append(bank)
+                if qd < 7:
+                    for k in range(4):
+                        second_pass(4 * (4 * qd + k) + o, bank, k)
+            if qd == 7:
                 for k in range(4):
-                    g = 4 * qd + k
-                    ch = 4 * g + o
-                    nc.tensor.matmul_mx(
-                        out=bank[:, P * k : P * k + P],
-                        lhsT=f_codes[:, P * ch : P * ch + P].bitcast(FP8X4),
-                        lhsT_scale=f_scales[:, P * ch : P * ch + P],
-                        rhs=g_codes[:, P * g : P * g + P].bitcast(FP8X4),
-                        rhs_scale=g_scales[:, P * g : P * g + P],
-                        start=True,
-                        stop=True,
-                    )
-                nc.scalar.copy(
-                    out=part(0, qd).rearrange("t (i k o b) -> t o k i b", i=4, k=4, o=4)[:, o],
-                    in_=bank[:].rearrange("t (k b i o) -> t o k i b", k=4, i=4, o=4)[:, o],
-                )
+                    for o in range(4):
+                        second_pass(4 * (4 * qd + k) + o, banks[o], k)
+            for o in range(4):
+                dst = part(0, qd).rearrange("t (i k o b) -> t o k i b", i=4, k=4, o=4)[:, o]
+                src = banks[o][:].rearrange("t (k b i o) -> t o k i b", k=4, i=4, o=4)[:, o]
+                if o < Y_ON_V[qd]:
+                    nc.vector.tensor_copy(out=dst, in_=src)
+                else:
+                    nc.scalar.copy(out=dst, in_=src)
 
         def back_and_norm(qd):
             ft = ps.tile([P, 512], F32, tag="bank", name="ft")
@@ -472,12 +486,12 @@ def tile_multiscale_gcn_pa_kernel(
                 feat_step(order[state["next"]])
 
         feats_until(4)
-        for i in range(10):
+        for i in range(8 + LAG + 1):
             if i < 8:
                 second_passes(i)
-            if 1 <= i <= 8:
-                back_and_norm(i - 1)
-            if i >= 2:
-                relu_and_store(i - 2)
+            if LAG <= i < 8 + LAG:
+                back_and_norm(i - LAG)
+            if i > LAG:
+                relu_and_store(i - LAG - 1)
             load_res(i + 2)
-            feats_until(min(N_TILES, max(4 * i + 8, first_left + ((i + 1) * left + 6) // 7)))
+            feats_until(min(N_TILES, max(4 * i + 8, first_left + ((i + 1) * left + SPAN - 1) // SPAN)))

@@ -17,14 +17,16 @@ S, CIN, COUT, V, T = 16, 512, 128, 32, 128
 EPS = 1e-5
 FLOPS = 2 * S * COUT * CIN * V * V + 2 * COUT * V * S * V * T
 N_TILES = COUT // 4
-RAW_BUFS = 7
-PLAN_W = "vvv"
-PLAN_T0 = {"s": 5}
+RAW_BUFS = 5
+PLAN_W = "vvs"
+PLAN_T0 = {"s": 5, "g": 2}
 PLAN_S1 = {"v": 5, "t": 2}
-PLAN_T1 = {"s": 5, "v": 1}
+PLAN_T1 = {"s": 5, "g": 2}
 PLAN_QG = {"s": 2, "t": 2}
-PLAN_END = "vsvsvss"
-Y_ON_V = (0, 0, 0, 0, 0, 0, 0, 2)
+PLAN_END = "vsvs"
+Y_ON_V = (0, 0, 0, 0, 0, 0, 0, 0)
+G_HOOKS = (0, 4, 9)
+RELU_S = 4
 SPAN = 6
 LAG = 1
 
@@ -34,7 +36,10 @@ def evenly(i, n, total):
 
 
 def spread(counts, total):
-    return ["".join(e for e in counts if evenly(i, counts[e], total)) for i in range(total)]
+    return [
+        "".join(e for e in counts if (evenly(i, counts[e], total) if e != "g" else i in G_HOOKS[: counts[e]]))
+        for i in range(total)
+    ]
 
 
 def tile_multiscale_gcn_pa_kernel(
@@ -139,22 +144,22 @@ def tile_multiscale_gcn_pa_kernel(
                     in_=src.rearrange("p (n t c i) -> p n c t i", n=n, t=4, i=4),
                 )
                 return
+            if engine == "s":
+                nc.scalar.copy(
+                    out=dst.rearrange("p (n c i t) -> p n c t i", n=n, i=4, t=4),
+                    in_=src.rearrange("p (n t c i) -> p n c t i", n=n, t=4, i=4),
+                )
+                return
             for b in range(n):
                 d, r = dst[:, w * b : w * b + w], src[:, w * b : w * b + w]
-                if engine == "s":
-                    nc.scalar.copy(
-                        out=d.rearrange("p (c i t) -> p c t i", i=4, t=4),
-                        in_=r.rearrange("p (t c i) -> p c t i", t=4, i=4),
-                    )
-                else:
-                    nc.gpsimd.tensor_scalar(
-                        out=d.rearrange("p (c t) -> p c t", t=4),
-                        in0=r.rearrange("p (t c) -> p c t", t=4),
-                        scalar1=1.0,
-                        scalar2=0.0,
-                        op0=ALU.mult,
-                        op1=ALU.add,
-                    )
+                nc.gpsimd.tensor_scalar(
+                    out=d.rearrange("p (c t) -> p c t", t=4),
+                    in0=r.rearrange("p (t c) -> p c t", t=4),
+                    scalar1=1.0,
+                    scalar2=0.0,
+                    op0=ALU.mult,
+                    op1=ALU.add,
+                )
 
         def quantise(codes, scales, c0, width, src):
             nc.vector.quantize_mx(
@@ -317,6 +322,8 @@ def tile_multiscale_gcn_pa_kernel(
                 )
                 feat_out_of_banks()
                 for e in plan[vl]:
+                    if e == "g" and len(slow) > 1:
+                        quantise_slow()
                     feat_step(e)
 
         x0 = big.tile([P, 8192], F32, tag="x", name="x0")
@@ -466,14 +473,19 @@ def tile_multiscale_gcn_pa_kernel(
             )
 
         def relu_and_store(qd):
-            nc.vector.tensor_scalar(
-                out=part(2, qd),
-                in0=part(1, qd),
-                scalar1=scsh[:, 8 + qd : 9 + qd],
-                scalar2=0.0,
-                op0=ALU.add,
-                op1=ALU.max,
-            )
+            if qd >= RELU_S:
+                nc.scalar.activation(
+                    out=part(2, qd), in_=part(1, qd), func=ACT.Relu, bias=scsh[:, 8 + qd : 9 + qd], scale=1.0
+                )
+            else:
+                nc.vector.tensor_scalar(
+                    out=part(2, qd),
+                    in0=part(1, qd),
+                    scalar1=scsh[:, 8 + qd : 9 + qd],
+                    scalar2=0.0,
+                    op0=ALU.add,
+                    op1=ALU.max,
+                )
             nc.sync.dma_start(out=out_v[qd], in_=part(2, qd))
 
         load_res(0)

@@ -18,6 +18,8 @@ EPS = 1e-5
 FLOPS = 2 * S * COUT * CIN * V * V + 2 * COUT * V * S * V * T
 N_TILES = COUT // 4
 RAW_BUFS = 5
+SPLIT = 24
+LAST_SPARE = 20
 PLAN_W = "vvs"
 PLAN_T0 = {"s": 5, "g": 2}
 PLAN_S1 = {"v": 5, "t": 2}
@@ -50,7 +52,7 @@ def tile_multiscale_gcn_pa_kernel(
         const = ctx.enter_context(tc.tile_pool(name="const", bufs=1))
         keep = ctx.enter_context(tc.tile_pool(name="keep", bufs=1))
         big = ctx.enter_context(tc.tile_pool(name="big", bufs=1))
-        raw_pool = ctx.enter_context(tc.tile_pool(name="rawp", bufs=RAW_BUFS))
+        raw_pool = ctx.enter_context(tc.tile_pool(name="rawp", bufs=1))
         grp_pool = ctx.enter_context(tc.tile_pool(name="grpp", bufs=4))
         slow_pool = ctx.enter_context(tc.tile_pool(name="slowp", bufs=2))
         res_pool = ctx.enter_context(tc.tile_pool(name="resp", bufs=3))
@@ -63,8 +65,19 @@ def tile_multiscale_gcn_pa_kernel(
         a_scales = keep.tile([P, V * V], U8, align_bytes=64)
         g_codes = keep.tile([P, COUT * V], U32, align_bytes=64)
         g_scales = keep.tile([P, COUT * V], U8, align_bytes=64)
-        f_codes = keep.tile([P, COUT * T], U32, align_bytes=64)
         f_scales = keep.tile([P, COUT * T], U8, align_bytes=64)
+        f_codes_a = keep.tile([P, SPLIT * 4 * T], U32, align_bytes=64)
+        spare = big.tile([P, 4 * 2048], BF16, tag="spare", name="spare", align_bytes=64)
+        early = big.tile([P, 5 * 2048], BF16, tag="in2", name="early", align_bytes=64)
+        f_codes_b = []
+
+        def feat_codes(ch, n):
+            if ch < 4 * SPLIT:
+                return f_codes_a[:, T * ch : T * (ch + n)]
+            if len(f_codes_b) == 0:
+                late_codes = big.tile([P, COUT * T - SPLIT * 4 * T], U32, tag="spare", name="late_codes", align_bytes=64)
+                f_codes_b.append(late_codes)
+            return f_codes_b[0][:, T * (ch - 4 * SPLIT) : T * (ch - 4 * SPLIT + n)]
 
         plan_t0 = spread(PLAN_T0, 16)
         plan_s1 = spread(PLAN_S1, 16)
@@ -93,21 +106,39 @@ def tile_multiscale_gcn_pa_kernel(
         a2 = ada_A.rearrange("n i v w -> (n i) (v w)")
         raws = {}
 
-        def load(kind, n):
+        ring_tile = raw_pool.tile([P, RAW_BUFS * 2048], BF16, name="ring_tile", align_bytes=64)
+        slow_ring = raw_pool.tile([P, 2 * 2048], BF16, name="slow_ring", align_bytes=64)
+        free = {
+            name: [tile[:, 2048 * k : 2048 * k + 2048] for k in range(n)]
+            for name, tile, n in (
+                ("early", early, 5), ("ring", ring_tile, RAW_BUFS), ("slow", slow_ring, 2), ("spare", spare, 4)
+            )
+        }
+        held = {}
+
+        def next_ring(kind, n):
+            if kind == "w" or (kind == "a" and n == 0):
+                return "early"
             if kind == "f" and order[n] == "g":
-                r = slow_pool.tile([P, 2048], BF16, tag="raws", name="raw_s")
-            else:
-                r = raw_pool.tile([P, 2048], BF16, tag="raw", name="raw")
+                return "slow"
+            if kind == "f" and n < LAST_SPARE and len(free["ring"]) == 0:
+                return "spare"
+            return "ring"
+
+        def load(kind, n):
+            ring = next_ring(kind, n)
+            r = free[ring].pop(0)
             raws[(kind, n)] = r
+            held[(kind, n)] = ring
             if kind == "a":
                 nc.sync.dma_start(
-                    out=r[:].rearrange("q (t c) -> q t c", t=4),
+                    out=r.rearrange("q (t c) -> q t c", t=4),
                     in_=a2[:, 512 * n : 512 * n + 512].rearrange("(q t) c -> q t c", t=4),
                 )
             elif kind == "w":
                 nc.sync.dma_start(
-                    out=r[:].rearrange("o (s i) -> o s i", s=4),
-                    in_=ada_w[4 * n : 4 * n + 4].rearrange("s o i -> o s i"),
+                    out=r,
+                    in_=ada_w[4 * n : 4 * n + 4].rearrange("s o i -> (s o) i").rearrange("(p r) i -> p (r i)", r=4),
                 )
             else:
                 for c in range(4):
@@ -120,14 +151,21 @@ def tile_multiscale_gcn_pa_kernel(
         loads.extend([("f", g) for g in range(2, N_TILES)])
         state = {"loaded": 0, "next": 0}
 
-        def load_next():
-            if state["loaded"] < len(loads):
+        def load_more():
+            while state["loaded"] < len(loads):
                 kind, n = loads[state["loaded"]]
+                if len(free[next_ring(kind, n)]) == 0:
+                    return
                 state["loaded"] += 1
                 load(kind, n)
 
-        for i in range(RAW_BUFS):
-            load_next()
+        def release(kind, n):
+            ring = held[(kind, n)]
+            if ring != "early":
+                free[ring].append(raws[(kind, n)])
+            load_more()
+
+        load_more()
 
         for row, vec in enumerate((bn_gamma, bn_beta, bn_mean, bn_var)):
             nc.scalar.dma_start(out=bn_rows[row : row + 1, :], in_=vec.unsqueeze(0))
@@ -171,26 +209,26 @@ def tile_multiscale_gcn_pa_kernel(
             if engine == "v":
                 nc.vector.tensor_copy(
                     out=g[:].rearrange("p (c i t) -> p c t i", i=4, t=4),
-                    in_=raws[("a", n)][:].rearrange("p (t c i) -> p c t i", t=4, i=4),
+                    in_=raws[("a", n)].rearrange("p (t c i) -> p c t i", t=4, i=4),
                 )
             else:
                 for b in range(4):
                     nc.gpsimd.tensor_scalar(
                         out=g[:, 512 * b : 512 * b + 512].rearrange("p (c t) -> p c t", t=4),
-                        in0=raws[("a", n)][:].rearrange("p (t b c) -> p b c t", t=4, b=4)[:, b],
+                        in0=raws[("a", n)].rearrange("p (t b c) -> p b c t", t=4, b=4)[:, b],
                         scalar1=1.0,
                         scalar2=0.0,
                         op0=ALU.mult,
                         op1=ALU.add,
                     )
-            load_next()
+            release("a", n)
             return g
 
         grp_a0 = regroup_a(0, "v")
         quantise(a_codes, a_scales, 0, 512, grp_a0[:])
 
         def w_transposes(c):
-            r32 = raws[("w", c)][:].bitcast(F32)
+            r32 = raws[("w", c)].bitcast(F32)
             g = grp_pool.tile([P, 2048], BF16, tag="grp", name="grp_w", align_bytes=64)
             g32 = g[:].bitcast(F32)
             banks = []
@@ -206,13 +244,13 @@ def tile_multiscale_gcn_pa_kernel(
                             ident32[:],
                         )
             for a in range(2):
-                dst = g32[:, 512 * a : 512 * a + 512].rearrange("q (b o u) -> q b o u", b=2, u=2)
-                src = banks[a][:].rearrange("q (b u o) -> q b o u", b=2, u=2)
+                dst = g32.rearrange("q (x a y) -> q a x y", a=2, y=4)[:, a]
+                src = banks[a][:].rearrange("q (y x) -> q x y", y=4)
                 if a == 0:
                     nc.scalar.copy(out=dst, in_=src)
                 else:
                     nc.vector.tensor_copy(out=dst, in_=src)
-            load_next()
+            release("w", c)
             return g
 
         grouped = {}
@@ -224,7 +262,11 @@ def tile_multiscale_gcn_pa_kernel(
         def quantise_tile(g):
             if g not in done:
                 done.add(g)
-                quantise(f_codes, f_scales, 512 * g, 512, grouped[g][:])
+                nc.vector.quantize_mx(
+                    out=feat_codes(4 * g, 4).bitcast(FP8X4),
+                    scales=f_scales[:, 512 * g : 512 * g + 512],
+                    in_=grouped[g][:],
+                )
 
         def quantise_waiting():
             for g in list(waiting):
@@ -239,7 +281,7 @@ def tile_multiscale_gcn_pa_kernel(
             g = state["next"]
             assert order[g] == engine
             state["next"] = g + 1
-            src = raws[("f", g)][:]
+            src = raws[("f", g)]
             if engine == "t":
                 banks = []
                 for half in range(2):
@@ -255,7 +297,7 @@ def tile_multiscale_gcn_pa_kernel(
                             stop=True,
                         )
                 in_banks.append((g, banks))
-                load_next()
+                release("f", g)
                 return
             if engine == "g":
                 gt = slow_pool.tile([P, 2048], BF16, tag="grps", name="grp_s", align_bytes=64)
@@ -263,7 +305,7 @@ def tile_multiscale_gcn_pa_kernel(
                 gt = grp_pool.tile([P, 2048], BF16, tag="grp", name="grp_f", align_bytes=64)
             grouped[g] = gt
             regroup(gt[:], src, 4, engine)
-            load_next()
+            release("f", g)
             if engine == "g":
                 slow.append(g)
             else:
@@ -425,7 +467,7 @@ def tile_multiscale_gcn_pa_kernel(
             g = ch // 4
             nc.tensor.matmul_mx(
                 out=bank[:, P * k : P * k + P],
-                lhsT=f_codes[:, P * ch : P * ch + P].bitcast(FP8X4),
+                lhsT=feat_codes(ch, 1).bitcast(FP8X4),
                 lhsT_scale=f_scales[:, P * ch : P * ch + P],
                 rhs=g_codes[:, P * g : P * g + P].bitcast(FP8X4),
                 rhs_scale=g_scales[:, P * g : P * g + P],

@@ -86,9 +86,10 @@ def tile_multiscale_gcn_pa_kernel(
         order = PLAN_W + "".join(plan_t0 + plan_s1 + plan_t1 + plan_qg) + PLAN_END
         assert len(order) == N_TILES
 
-        sq = const.tile([P, 2], F32)
-        nc.vector.memset(sq[:], 1.0)
-        nc.scalar.sqrt(out=sq[:, 1:2], in_=sq[:, 0:1])
+        minus_half = const.tile([P, 1], F32)
+        nc.gpsimd.memset(minus_half[:], -0.5)
+        warm = const.tile([P, 1], F32)
+        nc.scalar.activation(out=warm[:], in_=minus_half[:], func=ACT.Identity, bias=0.0, scale=1.0)
         b_rows = const.tile([P, P], BF16)
         nc.vector.memset(b_rows[:], 0.0)
         pa_rows = const.tile([P, S * V], BF16)
@@ -103,6 +104,8 @@ def tile_multiscale_gcn_pa_kernel(
         nc.scalar.dma_start(
             out=pa_rows[0:V, :].rearrange("v (s w) -> v s w", s=S), in_=PA.rearrange("s v w -> v s w")
         )
+        for row, vec in enumerate((bn_gamma, bn_beta, bn_mean, bn_var)):
+            nc.scalar.dma_start(out=bn_rows[row : row + 1, :], in_=vec.unsqueeze(0))
         a2 = ada_A.rearrange("n i v w -> (n i) (v w)")
         raws = {}
 
@@ -167,8 +170,6 @@ def tile_multiscale_gcn_pa_kernel(
 
         load_more()
 
-        for row, vec in enumerate((bn_gamma, bn_beta, bn_mean, bn_var)):
-            nc.scalar.dma_start(out=bn_rows[row : row + 1, :], in_=vec.unsqueeze(0))
         m16 = const.tile([P, 16], F32)
         nc.vector.tensor_reduce(
             out=m16[:], in_=ident32[:].rearrange("p (o v) -> p o v", o=16), axis=AX.X, op=ALU.add
@@ -398,6 +399,10 @@ def tile_multiscale_gcn_pa_kernel(
             for s in range(4 * c, 4 * c + 4):
                 add_bias(x0, s, accs[s - 4 * c])
             if c == 3:
+                zt = ps.tile([P, P], BF16, tag="bank", name="zt")
+                nc.tensor.transpose(zt[:], bn_rows[:], identb[:])
+                nc.scalar.copy(out=cst[:], in_=zt[:, 0:4])
+            if c == 3:
                 grp_a1 = regroup_a(1, "v")
             if c > 0:
                 for e in PLAN_W[c - 1]:
@@ -405,11 +410,20 @@ def tile_multiscale_gcn_pa_kernel(
         quantise(a_codes, a_scales, 512, 512, grp_a1[:])
         transposes_and_pa(0, x0, plan_t0)
         feat_out_of_banks()
-        zt = ps.tile([P, P], BF16, tag="bank", name="zt")
-        nc.tensor.transpose(zt[:], bn_rows[:], identb[:])
-        nc.vector.tensor_copy(out=cst[:], in_=zt[:, 0:4])
-        nc.vector.tensor_scalar_add(out=bn[:, 0:1], in0=cst[:, 3:4], scalar1=EPS)
-        nc.scalar.sqrt(out=sq[:, 1:2], in_=bn[:, 0:1])
+        nc.gpsimd.tensor_scalar_add(out=bn[:, 0:1], in0=cst[:, 3:4], scalar1=EPS)
+        nc.gpsimd.tensor_tensor(out=bn[:, 1:2], in0=bn[:, 0:1], in1=minus_half[:], op=ALU.pow)
+        nc.gpsimd.tensor_tensor(out=bn[:, 2:3], in0=cst[:, 0:1], in1=bn[:, 1:2], op=ALU.mult)
+        nc.gpsimd.tensor_tensor(out=bn[:, 3:4], in0=cst[:, 2:3], in1=bn[:, 2:3], op=ALU.mult)
+        nc.gpsimd.tensor_tensor(out=bn[:, 4:5], in0=cst[:, 1:2], in1=bn[:, 3:4], op=ALU.subtract)
+        for k in range(2):
+            nc.gpsimd.tensor_scalar(
+                out=rep[:, P * k : P * k + P],
+                in0=bn[:, 2 + 2 * k : 3 + 2 * k].to_broadcast([P, P]),
+                scalar1=1.0,
+                scalar2=0.0,
+                op0=ALU.mult,
+                op1=ALU.add,
+            )
         x1 = big.tile([P, 8192], F32, tag="x", name="x1")
         for s in range(S):
             add_bias(x1, s, first_pass(1, s))
@@ -418,13 +432,6 @@ def tile_multiscale_gcn_pa_kernel(
             feat_out_of_banks()
             for e in plan_s1[s]:
                 feat_step(e)
-            if s == 5:
-                nc.vector.reciprocal(out=bn[:, 1:2], in_=sq[:, 1:2])
-                nc.vector.tensor_tensor(out=bn[:, 2:3], in0=cst[:, 0:1], in1=bn[:, 1:2], op=ALU.mult)
-                nc.vector.tensor_tensor(out=bn[:, 3:4], in0=cst[:, 2:3], in1=bn[:, 2:3], op=ALU.mult)
-                nc.vector.tensor_tensor(out=bn[:, 4:5], in0=cst[:, 1:2], in1=bn[:, 3:4], op=ALU.subtract)
-                nc.vector.tensor_copy(out=rep[:, 0:P], in_=bn[:, 2:3].to_broadcast([P, P]))
-                nc.vector.tensor_copy(out=rep[:, P : 2 * P], in_=bn[:, 4:5].to_broadcast([P, P]))
             if s == 10:
                 rt = ps.tile([P, 2 * P], F32, tag="bank", name="rt")
                 nc.tensor.transpose(rt[:, 0:P], rep[:, 0:P], ident32[:])

@@ -10,7 +10,6 @@ U8 = mybir.dt.uint8
 FP8X4 = mybir.dt.float8_e4m3fn_x4
 ALU = mybir.AluOpType
 ACT = mybir.ActivationFunctionType
-AX = mybir.AxisListType
 
 P = 128
 S, CIN, COUT, V, T = 16, 512, 128, 32, 128
@@ -19,18 +18,20 @@ FLOPS = 2 * S * COUT * CIN * V * V + 2 * COUT * V * S * V * T
 N_TILES = COUT // 4
 RAW_BUFS = 5
 SPLIT = 24
-LAST_SPARE = 20
-PLAN_W = "vvs"
+PLAN_H = ""
+PLAN_W = "vvv"
+W_FIRST = False
+LOADS = "a0 w0 s0 s1 w1 w2 f0 w3 s2 f1 a1"
 PLAN_T0 = {"s": 5, "g": 2}
 PLAN_S1 = {"v": 5, "t": 2}
 PLAN_T1 = {"s": 5, "g": 2}
-PLAN_QG = {"s": 2, "t": 2}
-PLAN_END = "vsvs"
+PLAN_TAIL = ("ts", "ts", "v", "s", "v", "s")
 Y_ON_V = (0, 0, 0, 0, 0, 0, 0, 0)
+LAST_SPARE = N_TILES - len("".join(PLAN_TAIL))
 G_HOOKS = (0, 4, 9)
 RELU_S = 4
-SPAN = 6
-LAG = 1
+LAG = 2
+AHEAD = 2
 
 
 def evenly(i, n, total):
@@ -55,7 +56,6 @@ def tile_multiscale_gcn_pa_kernel(
         raw_pool = ctx.enter_context(tc.tile_pool(name="rawp", bufs=1))
         grp_pool = ctx.enter_context(tc.tile_pool(name="grpp", bufs=4))
         slow_pool = ctx.enter_context(tc.tile_pool(name="slowp", bufs=2))
-        res_pool = ctx.enter_context(tc.tile_pool(name="resp", bufs=3))
         ps = ctx.enter_context(tc.psum_pool(name="ps", bufs=8))
         ctx.enter_context(tc.manual_schedule())
 
@@ -63,10 +63,10 @@ def tile_multiscale_gcn_pa_kernel(
         w_scales = keep.tile([P, S * COUT], U8, align_bytes=64)
         a_codes = keep.tile([P, V * V], U32, align_bytes=64)
         a_scales = keep.tile([P, V * V], U8, align_bytes=64)
-        g_codes = keep.tile([P, COUT * V], U32, align_bytes=64)
         g_scales = keep.tile([P, COUT * V], U8, align_bytes=64)
         f_scales = keep.tile([P, COUT * T], U8, align_bytes=64)
         f_codes_a = keep.tile([P, SPLIT * 4 * T], U32, align_bytes=64)
+        spare_g = big.tile([P, 4 * 2048], BF16, tag="g", name="spare_g", align_bytes=64)
         spare = big.tile([P, 4 * 2048], BF16, tag="spare", name="spare", align_bytes=64)
         early = big.tile([P, 5 * 2048], BF16, tag="in2", name="early", align_bytes=64)
         f_codes_b = []
@@ -82,14 +82,13 @@ def tile_multiscale_gcn_pa_kernel(
         plan_t0 = spread(PLAN_T0, 16)
         plan_s1 = spread(PLAN_S1, 16)
         plan_t1 = spread(PLAN_T1, 16)
-        plan_qg = spread(PLAN_QG, 4)
-        order = PLAN_W + "".join(plan_t0 + plan_s1 + plan_t1 + plan_qg) + PLAN_END
+        order = PLAN_H + PLAN_W + "".join(plan_t0 + plan_s1 + plan_t1) + "".join(PLAN_TAIL)
         assert len(order) == N_TILES
 
-        minus_half = const.tile([P, 1], F32)
+        minus_half = const.tile([P, 8], F32)
         nc.gpsimd.memset(minus_half[:], -0.5)
         warm = const.tile([P, 1], F32)
-        nc.scalar.activation(out=warm[:], in_=minus_half[:], func=ACT.Identity, bias=0.0, scale=1.0)
+        nc.scalar.activation(out=warm[:], in_=minus_half[:, 0:1], func=ACT.Identity, bias=0.0, scale=1.0)
         b_rows = const.tile([P, P], BF16)
         nc.vector.memset(b_rows[:], 0.0)
         pa_rows = const.tile([P, S * V], BF16)
@@ -100,12 +99,6 @@ def tile_multiscale_gcn_pa_kernel(
         make_identity(nc, ident32[:])
         identb = const.tile([P, P], BF16)
         make_identity(nc, identb[:])
-        nc.scalar.dma_start(out=b_rows[0:S, :], in_=ada_b)
-        nc.scalar.dma_start(
-            out=pa_rows[0:V, :].rearrange("v (s w) -> v s w", s=S), in_=PA.rearrange("s v w -> v s w")
-        )
-        for row, vec in enumerate((bn_gamma, bn_beta, bn_mean, bn_var)):
-            nc.scalar.dma_start(out=bn_rows[row : row + 1, :], in_=vec.unsqueeze(0))
         a2 = ada_A.rearrange("n i v w -> (n i) (v w)")
         raws = {}
 
@@ -114,7 +107,8 @@ def tile_multiscale_gcn_pa_kernel(
         free = {
             name: [tile[:, 2048 * k : 2048 * k + 2048] for k in range(n)]
             for name, tile, n in (
-                ("early", early, 5), ("ring", ring_tile, RAW_BUFS), ("slow", slow_ring, 2), ("spare", spare, 4)
+                ("early", early, 5), ("ring", ring_tile, RAW_BUFS), ("slow", slow_ring, 2), ("spare", spare, 4),
+                ("spare_g", spare_g, 4)
             )
         }
         held = {}
@@ -122,9 +116,11 @@ def tile_multiscale_gcn_pa_kernel(
         def next_ring(kind, n):
             if kind == "w" or (kind == "a" and n == 0):
                 return "early"
-            if kind == "f" and order[n] == "g":
+            if kind == "f" and order[n] == "g" and len(free["slow"]) > 0:
                 return "slow"
             if kind == "f" and n < LAST_SPARE and len(free["ring"]) == 0:
+                if len(free["spare"]) == 0:
+                    return "spare_g"
                 return "spare"
             return "ring"
 
@@ -150,13 +146,28 @@ def tile_multiscale_gcn_pa_kernel(
                         in_=feat[:, 0, 4 * n + c].rearrange("s (q j) t -> s q (j t)", j=4),
                     )
 
-        loads = [("a", 0), ("w", 0), ("w", 1), ("w", 2), ("f", 0), ("w", 3), ("f", 1), ("a", 1)]
-        loads.extend([("f", g) for g in range(2, N_TILES)])
+        loads = [(x[0], int(x[1:])) for x in LOADS.split(" ")]
+        loads.extend([("f", g) for g in range(len([x for x in loads if x[0] == "f"]), N_TILES)])
         state = {"loaded": 0, "next": 0}
+
+        def load_small(n):
+            if n == 0:
+                nc.scalar.dma_start(out=b_rows[0:S, :], in_=ada_b)
+            elif n == 1:
+                nc.scalar.dma_start(
+                    out=pa_rows[0:V, :].rearrange("v (s w) -> v s w", s=S), in_=PA.rearrange("s v w -> v s w")
+                )
+            else:
+                for row, vec in enumerate((bn_gamma, bn_beta, bn_mean, bn_var)):
+                    nc.sync.dma_start(out=bn_rows[row : row + 1, :], in_=vec.unsqueeze(0))
 
         def load_more():
             while state["loaded"] < len(loads):
                 kind, n = loads[state["loaded"]]
+                if kind == "s":
+                    state["loaded"] += 1
+                    load_small(n)
+                    continue
                 if len(free[next_ring(kind, n)]) == 0:
                     return
                 state["loaded"] += 1
@@ -169,11 +180,6 @@ def tile_multiscale_gcn_pa_kernel(
             load_more()
 
         load_more()
-
-        m16 = const.tile([P, 16], F32)
-        nc.vector.tensor_reduce(
-            out=m16[:], in_=ident32[:].rearrange("p (o v) -> p o v", o=16), axis=AX.X, op=ALU.add
-        )
 
         def regroup(dst, src, n, engine):
             w = 2048 // n
@@ -225,8 +231,6 @@ def tile_multiscale_gcn_pa_kernel(
             release("a", n)
             return g
 
-        grp_a0 = regroup_a(0, "v")
-        quantise(a_codes, a_scales, 0, 512, grp_a0[:])
 
         def w_transposes(c):
             r32 = raws[("w", c)].bitcast(F32)
@@ -370,18 +374,37 @@ def tile_multiscale_gcn_pa_kernel(
                     feat_step(e)
 
         x0 = big.tile([P, 8192], F32, tag="x", name="x0")
-        grp_w = w_transposes(0)
-        quantise(w_codes, w_scales, 0, 512, grp_w[:])
+        for e in PLAN_H:
+            feat_step(e)
+        if W_FIRST:
+            grp_w = w_transposes(0)
+            grp_a0 = regroup_a(0, "v")
+            quantise(w_codes, w_scales, 0, 512, grp_w[:])
+            quantise(a_codes, a_scales, 0, 512, grp_a0[:])
+        else:
+            grp_a0 = regroup_a(0, "v")
+            quantise(a_codes, a_scales, 0, 512, grp_a0[:])
+            grp_w = w_transposes(0)
+            quantise(w_codes, w_scales, 0, 512, grp_w[:])
         bt = ps.tile([P, P], BF16, tag="bank", name="bt")
         nc.tensor.transpose(bt[:], b_rows[:], identb[:])
         bias = const.tile([P, S], F32)
         nc.vector.tensor_copy(out=bias[:], in_=bt[:, 0:S])
-        cst = const.tile([P, 4], F32)
-        bn = const.tile([P, 8], F32)
-        rep = const.tile([P, 2 * P], F32)
+        cst = const.tile([P, 32], F32)
+        bn = const.tile([P, 24], F32)
         scsh = const.tile([P, 16], F32)
-        bn_sel = const.tile([P, 2 * P], F32)
+        bn_rep = const.tile([P, 8 * P], BF16)
+        nc.gpsimd.tensor_scalar(
+            out=bn_rep[:].rearrange("p (o k) -> p o k", k=8),
+            in0=bn_rows[:].unsqueeze(2).to_broadcast([P, P, 8]),
+            scalar1=1.0,
+            scalar2=0.0,
+            op0=ALU.mult,
+            op1=ALU.add,
+        )
         for c in range(4):
+            if c in (1, 2):
+                feat_step(PLAN_W[c - 1])
             if c < 3:
                 grp_w = w_transposes(c + 1)
             if c == 0:
@@ -399,31 +422,25 @@ def tile_multiscale_gcn_pa_kernel(
             for s in range(4 * c, 4 * c + 4):
                 add_bias(x0, s, accs[s - 4 * c])
             if c == 3:
-                zt = ps.tile([P, P], BF16, tag="bank", name="zt")
-                nc.tensor.transpose(zt[:], bn_rows[:], identb[:])
-                nc.scalar.copy(out=cst[:], in_=zt[:, 0:4])
+                zt = ps.tile([P, 8 * P], BF16, tag="bank", name="zt")
+                for k in range(8):
+                    nc.tensor.transpose(zt[:, P * k : P * k + P], bn_rep[:, P * k : P * k + P], identb[:])
+                nc.scalar.copy(
+                    out=cst[:].rearrange("p (r c) -> p r c", r=4),
+                    in_=zt[:].rearrange("p (c r) -> p r c", c=8)[:, 0:4, :],
+                )
             if c == 3:
                 grp_a1 = regroup_a(1, "v")
-            if c > 0:
-                for e in PLAN_W[c - 1]:
-                    feat_step(e)
         quantise(a_codes, a_scales, 512, 512, grp_a1[:])
+        for e in PLAN_W[2:]:
+            feat_step(e)
         transposes_and_pa(0, x0, plan_t0)
         feat_out_of_banks()
-        nc.gpsimd.tensor_scalar_add(out=bn[:, 0:1], in0=cst[:, 3:4], scalar1=EPS)
-        nc.gpsimd.tensor_tensor(out=bn[:, 1:2], in0=bn[:, 0:1], in1=minus_half[:], op=ALU.pow)
-        nc.gpsimd.tensor_tensor(out=bn[:, 2:3], in0=cst[:, 0:1], in1=bn[:, 1:2], op=ALU.mult)
-        nc.gpsimd.tensor_tensor(out=bn[:, 3:4], in0=cst[:, 2:3], in1=bn[:, 2:3], op=ALU.mult)
-        nc.gpsimd.tensor_tensor(out=bn[:, 4:5], in0=cst[:, 1:2], in1=bn[:, 3:4], op=ALU.subtract)
-        for k in range(2):
-            nc.gpsimd.tensor_scalar(
-                out=rep[:, P * k : P * k + P],
-                in0=bn[:, 2 + 2 * k : 3 + 2 * k].to_broadcast([P, P]),
-                scalar1=1.0,
-                scalar2=0.0,
-                op0=ALU.mult,
-                op1=ALU.add,
-            )
+        nc.gpsimd.tensor_scalar_add(out=bn[:, 0:8], in0=cst[:, 24:32], scalar1=EPS)
+        nc.gpsimd.tensor_tensor(out=bn[:, 8:16], in0=bn[:, 0:8], in1=minus_half[:], op=ALU.pow)
+        nc.gpsimd.tensor_tensor(out=scsh[:, 0:8], in0=cst[:, 0:8], in1=bn[:, 8:16], op=ALU.mult)
+        nc.gpsimd.tensor_tensor(out=bn[:, 16:24], in0=cst[:, 16:24], in1=scsh[:, 0:8], op=ALU.mult)
+        nc.gpsimd.tensor_tensor(out=scsh[:, 8:16], in0=cst[:, 8:16], in1=bn[:, 16:24], op=ALU.subtract)
         x1 = big.tile([P, 8192], F32, tag="x", name="x1")
         for s in range(S):
             add_bias(x1, s, first_pass(1, s))
@@ -432,29 +449,8 @@ def tile_multiscale_gcn_pa_kernel(
             feat_out_of_banks()
             for e in plan_s1[s]:
                 feat_step(e)
-            if s == 10:
-                rt = ps.tile([P, 2 * P], F32, tag="bank", name="rt")
-                nc.tensor.transpose(rt[:, 0:P], rep[:, 0:P], ident32[:])
-                nc.tensor.transpose(rt[:, P : 2 * P], rep[:, P : 2 * P], ident32[:])
-                nc.vector.tensor_tensor(
-                    out=bn_sel[:].rearrange("p (c o) -> p c o", o=16),
-                    in0=rt[:].rearrange("p (c o) -> p c o", o=16),
-                    in1=m16[:].unsqueeze(1).to_broadcast([P, 16, 16]),
-                    op=ALU.mult,
-                )
-                nc.vector.tensor_reduce(
-                    out=scsh[:], in_=bn_sel[:].rearrange("p (c o) -> p c o", o=16), axis=AX.X, op=ALU.add
-                )
         transposes_and_pa(1, x1, plan_t1)
         feat_out_of_banks()
-        for c in range(4):
-            quantise(g_codes, g_scales, 1024 * c, 1024, in2[:, 4096 * c : 4096 * c + 4096])
-            quantise_slow()
-            feat_out_of_banks()
-            for e in plan_qg[c]:
-                feat_step(e)
-        feat_out_of_banks()
-
         res_v = res.rearrange("n o v t -> (n o v t)").rearrange("(g p f) -> g p f", p=P, f=512)
         out_v = out.rearrange("n o v t -> (n o v t)").rearrange("(g p f) -> g p f", p=P, f=512)
         late = big.tile([P, 8192], F32, tag="x", name="late")
@@ -462,12 +458,13 @@ def tile_multiscale_gcn_pa_kernel(
 
         def load_res(qd):
             if qd < 8:
-                r = res_pool.tile([P, 512], BF16, tag="res", name="res_t")
-                nc.sync.dma_start(out=r[:], in_=res_v[qd])
+                c0 = 6144 + 256 * qd
+                r = late[:, c0 : c0 + 256].bitcast(BF16)
+                nc.sync.dma_start(out=r, in_=res_v[qd])
                 res_tiles[qd] = r
 
         def part(kind, qd):
-            c0 = 2048 * kind + 512 * (qd % 3)
+            c0 = 2048 * kind + 512 * (qd % 4)
             return late[:, c0 : c0 + 512]
 
         def second_pass(ch, bank, k):
@@ -506,53 +503,59 @@ def tile_multiscale_gcn_pa_kernel(
                 else:
                     nc.scalar.copy(out=dst, in_=src)
 
+        def halves(qd):
+            return ((0, 2), (2, 4)) if qd == 7 else ((0, 4),)
+
         def back_and_norm(qd):
-            ft = ps.tile([P, 512], F32, tag="bank", name="ft")
-            for i in range(4):
-                nc.tensor.transpose(
-                    ft[:, P * i : P * i + P], part(0, qd)[:, P * i : P * i + P], ident32[:]
+            for i0, i1 in halves(qd):
+                ft = ps.tile([P, 512], F32, tag="bank", name="ft")
+                for i in range(i0, i1):
+                    nc.tensor.transpose(
+                        ft[:, P * (i - i0) : P * (i - i0) + P], part(0, qd)[:, P * i : P * i + P], ident32[:]
+                    )
+                nc.vector.scalar_tensor_tensor(
+                    out=part(1, qd)[:, P * i0 : P * i1],
+                    in0=ft[:, 0 : P * (i1 - i0)],
+                    scalar=scsh[:, qd : qd + 1],
+                    in1=res_tiles[qd][:, P * i0 : P * i1],
+                    op0=ALU.mult,
+                    op1=ALU.add,
                 )
-            nc.vector.scalar_tensor_tensor(
-                out=part(1, qd),
-                in0=ft[:],
-                scalar=scsh[:, qd : qd + 1],
-                in1=res_tiles[qd][:],
-                op0=ALU.mult,
-                op1=ALU.add,
-            )
 
         def relu_and_store(qd):
-            if qd >= RELU_S:
-                nc.scalar.activation(
-                    out=part(2, qd), in_=part(1, qd), func=ACT.Relu, bias=scsh[:, 8 + qd : 9 + qd], scale=1.0
-                )
-            else:
-                nc.vector.tensor_scalar(
-                    out=part(2, qd),
-                    in0=part(1, qd),
-                    scalar1=scsh[:, 8 + qd : 9 + qd],
-                    scalar2=0.0,
-                    op0=ALU.add,
-                    op1=ALU.max,
-                )
-            nc.sync.dma_start(out=out_v[qd], in_=part(2, qd))
+            for i0, i1 in halves(qd):
+                z = part(1, qd)[:, P * i0 : P * i1]
+                r = part(2, qd)[:, P * i0 : P * i1]
+                if qd >= RELU_S:
+                    nc.scalar.activation(out=r, in_=z, func=ACT.Relu, bias=scsh[:, 8 + qd : 9 + qd], scale=1.0)
+                else:
+                    nc.vector.tensor_scalar(
+                        out=r,
+                        in0=z,
+                        scalar1=scsh[:, 8 + qd : 9 + qd],
+                        scalar2=0.0,
+                        op0=ALU.add,
+                        op1=ALU.max,
+                    )
+                nc.sync.dma_start(out=out_v[qd][:, P * i0 : P * i1], in_=r)
 
-        load_res(0)
-        load_res(1)
-        first_left = state["next"]
-        left = N_TILES - first_left
-
-        def feats_until(want):
-            while state["next"] < want:
-                feat_step(order[state["next"]])
-
-        feats_until(4)
-        for i in range(8 + LAG + 1):
-            if i < 8:
-                second_passes(i)
-            if LAG <= i < 8 + LAG:
-                back_and_norm(i - LAG)
-            if i > LAG:
-                relu_and_store(i - LAG - 1)
-            load_res(i + 2)
-            feats_until(min(N_TILES, max(4 * i + 8, first_left + ((i + 1) * left + SPAN - 1) // SPAN)))
+        for qd in range(AHEAD):
+            load_res(qd)
+        g_codes = big.tile([P, COUT * V], U32, tag="g", name="g_codes", align_bytes=64)
+        for i in range(9 + LAG + 1):
+            if i < 4:
+                quantise(g_codes, g_scales, 1024 * i, 1024, in2[:, 4096 * i : 4096 * i + 4096])
+                quantise_slow()
+            feat_out_of_banks()
+            if 1 <= i < 9:
+                second_passes(i - 1)
+            if i > len(PLAN_TAIL):
+                quantise_waiting()
+            if 1 + LAG <= i < 9 + LAG:
+                back_and_norm(i - LAG - 1)
+            if i > LAG + 1:
+                relu_and_store(i - LAG - 2)
+            load_res(i + AHEAD)
+            if i < len(PLAN_TAIL):
+                for e in PLAN_TAIL[i]:
+                    feat_step(e)

from contextlib import ExitStack

import concourse.mybir as mybir
from concourse.masks import make_identity

F32 = mybir.dt.float32
BF16 = mybir.dt.bfloat16
U32 = mybir.dt.uint32
U8 = mybir.dt.uint8
FP8X4 = mybir.dt.float8_e4m3fn_x4
ALU = mybir.AluOpType
ACT = mybir.ActivationFunctionType

P = 128
S, CIN, COUT, V, T = 16, 512, 128, 32, 128
EPS = 1e-5
FLOPS = 2 * S * COUT * CIN * V * V + 2 * COUT * V * S * V * T
N_TILES = COUT // 4
RAW_BUFS = 5
SPLIT = 24
PLAN_H = ""
PLAN_W = "vvv"
W_FIRST = False
LOADS = "a0 w0 s0 s1 w1 w2 f0 w3 s2 f1 a1"
PLAN_T0 = {"s": 5, "g": 2}
PLAN_S1 = {"v": 5, "t": 2}
PLAN_T1 = {"s": 5, "g": 2}
PLAN_TAIL = ("ts", "ts", "v", "s", "v", "s")
Y_ON_V = (0, 0, 0, 0, 0, 0, 0, 0)
LAST_SPARE = N_TILES - len("".join(PLAN_TAIL))
G_HOOKS = (0, 4, 9)
RELU_S = 4
LAG = 2
AHEAD = 2


def evenly(i, n, total):
    return (i + 1) * n // total > i * n // total


def spread(counts, total):
    return [
        "".join(e for e in counts if (evenly(i, counts[e], total) if e != "g" else i in G_HOOKS[: counts[e]]))
        for i in range(total)
    ]


def tile_multiscale_gcn_pa_kernel(
    tc, ada_A, ada_w, ada_b, PA, feat, bn_gamma, bn_beta, bn_mean, bn_var, res, out
):
    nc = tc.nc
    with ExitStack() as ctx:
        const = ctx.enter_context(tc.tile_pool(name="const", bufs=1))
        keep = ctx.enter_context(tc.tile_pool(name="keep", bufs=1))
        big = ctx.enter_context(tc.tile_pool(name="big", bufs=1))
        raw_pool = ctx.enter_context(tc.tile_pool(name="rawp", bufs=1))
        grp_pool = ctx.enter_context(tc.tile_pool(name="grpp", bufs=4))
        slow_pool = ctx.enter_context(tc.tile_pool(name="slowp", bufs=2))
        ps = ctx.enter_context(tc.psum_pool(name="ps", bufs=8))
        ctx.enter_context(tc.manual_schedule())

        w_codes = keep.tile([P, S * COUT], U32, align_bytes=64)
        w_scales = keep.tile([P, S * COUT], U8, align_bytes=64)
        a_codes = keep.tile([P, V * V], U32, align_bytes=64)
        a_scales = keep.tile([P, V * V], U8, align_bytes=64)
        g_scales = keep.tile([P, COUT * V], U8, align_bytes=64)
        f_scales = keep.tile([P, COUT * T], U8, align_bytes=64)
        f_codes_a = keep.tile([P, SPLIT * 4 * T], U32, align_bytes=64)
        spare_g = big.tile([P, 4 * 2048], BF16, tag="g", name="spare_g", align_bytes=64)
        spare = big.tile([P, 4 * 2048], BF16, tag="spare", name="spare", align_bytes=64)
        early = big.tile([P, 5 * 2048], BF16, tag="in2", name="early", align_bytes=64)
        f_codes_b = []

        def feat_codes(ch, n):
            if ch < 4 * SPLIT:
                return f_codes_a[:, T * ch : T * (ch + n)]
            if len(f_codes_b) == 0:
                late_codes = big.tile([P, COUT * T - SPLIT * 4 * T], U32, tag="spare", name="late_codes", align_bytes=64)
                f_codes_b.append(late_codes)
            return f_codes_b[0][:, T * (ch - 4 * SPLIT) : T * (ch - 4 * SPLIT + n)]

        plan_t0 = spread(PLAN_T0, 16)
        plan_s1 = spread(PLAN_S1, 16)
        plan_t1 = spread(PLAN_T1, 16)
        order = PLAN_H + PLAN_W + "".join(plan_t0 + plan_s1 + plan_t1) + "".join(PLAN_TAIL)
        assert len(order) == N_TILES

        minus_half = const.tile([P, 8], F32)
        nc.gpsimd.memset(minus_half[:], -0.5)
        warm = const.tile([P, 1], F32)
        nc.scalar.activation(out=warm[:], in_=minus_half[:, 0:1], func=ACT.Identity, bias=0.0, scale=1.0)
        b_rows = const.tile([P, P], BF16)
        nc.vector.memset(b_rows[:], 0.0)
        pa_rows = const.tile([P, S * V], BF16)
        nc.vector.memset(pa_rows[:], 0.0)
        bn_rows = const.tile([P, P], BF16)
        nc.vector.memset(bn_rows[:], 0.0)
        ident32 = const.tile([P, P], F32)
        make_identity(nc, ident32[:])
        identb = const.tile([P, P], BF16)
        make_identity(nc, identb[:])
        a2 = ada_A.rearrange("n i v w -> (n i) (v w)")
        raws = {}

        ring_tile = raw_pool.tile([P, RAW_BUFS * 2048], BF16, name="ring_tile", align_bytes=64)
        slow_ring = raw_pool.tile([P, 2 * 2048], BF16, name="slow_ring", align_bytes=64)
        free = {
            name: [tile[:, 2048 * k : 2048 * k + 2048] for k in range(n)]
            for name, tile, n in (
                ("early", early, 5), ("ring", ring_tile, RAW_BUFS), ("slow", slow_ring, 2), ("spare", spare, 4),
                ("spare_g", spare_g, 4)
            )
        }
        held = {}

        def next_ring(kind, n):
            if kind == "w" or (kind == "a" and n == 0):
                return "early"
            if kind == "f" and order[n] == "g" and len(free["slow"]) > 0:
                return "slow"
            if kind == "f" and n < LAST_SPARE and len(free["ring"]) == 0:
                if len(free["spare"]) == 0:
                    return "spare_g"
                return "spare"
            return "ring"

        def load(kind, n):
            ring = next_ring(kind, n)
            r = free[ring].pop(0)
            raws[(kind, n)] = r
            held[(kind, n)] = ring
            if kind == "a":
                nc.sync.dma_start(
                    out=r.rearrange("q (t c) -> q t c", t=4),
                    in_=a2[:, 512 * n : 512 * n + 512].rearrange("(q t) c -> q t c", t=4),
                )
            elif kind == "w":
                nc.sync.dma_start(
                    out=r,
                    in_=ada_w[4 * n : 4 * n + 4].rearrange("s o i -> (s o) i").rearrange("(p r) i -> p (r i)", r=4),
                )
            else:
                for c in range(4):
                    nc.sync.dma_start(
                        out=r[:, 512 * c : 512 * c + 512],
                        in_=feat[:, 0, 4 * n + c].rearrange("s (q j) t -> s q (j t)", j=4),
                    )

        loads = [(x[0], int(x[1:])) for x in LOADS.split(" ")]
        loads.extend([("f", g) for g in range(len([x for x in loads if x[0] == "f"]), N_TILES)])
        state = {"loaded": 0, "next": 0}

        def load_small(n):
            if n == 0:
                nc.scalar.dma_start(out=b_rows[0:S, :], in_=ada_b)
            elif n == 1:
                nc.scalar.dma_start(
                    out=pa_rows[0:V, :].rearrange("v (s w) -> v s w", s=S), in_=PA.rearrange("s v w -> v s w")
                )
            else:
                for row, vec in enumerate((bn_gamma, bn_beta, bn_mean, bn_var)):
                    nc.sync.dma_start(out=bn_rows[row : row + 1, :], in_=vec.unsqueeze(0))

        def load_more():
            while state["loaded"] < len(loads):
                kind, n = loads[state["loaded"]]
                if kind == "s":
                    state["loaded"] += 1
                    load_small(n)
                    continue
                if len(free[next_ring(kind, n)]) == 0:
                    return
                state["loaded"] += 1
                load(kind, n)

        def release(kind, n):
            ring = held[(kind, n)]
            if ring != "early":
                free[ring].append(raws[(kind, n)])
            load_more()

        load_more()

        def regroup(dst, src, n, engine):
            w = 2048 // n
            if engine == "v":
                nc.vector.tensor_copy(
                    out=dst.rearrange("p (n c i t) -> p n c t i", n=n, i=4, t=4),
                    in_=src.rearrange("p (n t c i) -> p n c t i", n=n, t=4, i=4),
                )
                return
            if engine == "s":
                nc.scalar.copy(
                    out=dst.rearrange("p (n c i t) -> p n c t i", n=n, i=4, t=4),
                    in_=src.rearrange("p (n t c i) -> p n c t i", n=n, t=4, i=4),
                )
                return
            for b in range(n):
                d, r = dst[:, w * b : w * b + w], src[:, w * b : w * b + w]
                nc.gpsimd.tensor_scalar(
                    out=d.rearrange("p (c t) -> p c t", t=4),
                    in0=r.rearrange("p (t c) -> p c t", t=4),
                    scalar1=1.0,
                    scalar2=0.0,
                    op0=ALU.mult,
                    op1=ALU.add,
                )

        def quantise(codes, scales, c0, width, src):
            nc.vector.quantize_mx(
                out=codes[:, c0 : c0 + width].bitcast(FP8X4), scales=scales[:, c0 : c0 + width], in_=src
            )

        def regroup_a(n, engine):
            g = grp_pool.tile([P, 2048], BF16, tag="grp", name="grp_a", align_bytes=64)
            if engine == "v":
                nc.vector.tensor_copy(
                    out=g[:].rearrange("p (c i t) -> p c t i", i=4, t=4),
                    in_=raws[("a", n)].rearrange("p (t c i) -> p c t i", t=4, i=4),
                )
            else:
                for b in range(4):
                    nc.gpsimd.tensor_scalar(
                        out=g[:, 512 * b : 512 * b + 512].rearrange("p (c t) -> p c t", t=4),
                        in0=raws[("a", n)].rearrange("p (t b c) -> p b c t", t=4, b=4)[:, b],
                        scalar1=1.0,
                        scalar2=0.0,
                        op0=ALU.mult,
                        op1=ALU.add,
                    )
            release("a", n)
            return g


        def w_transposes(c):
            r32 = raws[("w", c)].bitcast(F32)
            g = grp_pool.tile([P, 2048], BF16, tag="grp", name="grp_w", align_bytes=64)
            g32 = g[:].bitcast(F32)
            banks = []
            for a in range(2):
                wt = ps.tile([P, 512], F32, tag="bank", name="wt")
                banks.append(wt)
                for b in range(2):
                    for u in range(2):
                        col = (2 * a + b) * 256
                        nc.tensor.transpose(
                            wt[:, (2 * b + u) * 128 : (2 * b + u) * 128 + 128],
                            r32[:, col + u : col + 256 : 2],
                            ident32[:],
                        )
            for a in range(2):
                dst = g32.rearrange("q (x a y) -> q a x y", a=2, y=4)[:, a]
                src = banks[a][:].rearrange("q (y x) -> q x y", y=4)
                if a == 0:
                    nc.scalar.copy(out=dst, in_=src)
                else:
                    nc.vector.tensor_copy(out=dst, in_=src)
            release("w", c)
            return g

        grouped = {}
        waiting = []
        slow = []
        in_banks = []
        done = set()

        def quantise_tile(g):
            if g not in done:
                done.add(g)
                nc.vector.quantize_mx(
                    out=feat_codes(4 * g, 4).bitcast(FP8X4),
                    scales=f_scales[:, 512 * g : 512 * g + 512],
                    in_=grouped[g][:],
                )

        def quantise_waiting():
            for g in list(waiting):
                quantise_tile(g)
            waiting.clear()

        def quantise_slow():
            if len(slow) > 0:
                quantise_tile(slow.pop(0))

        def feat_step(engine):
            g = state["next"]
            assert order[g] == engine
            state["next"] = g + 1
            src = raws[("f", g)]
            if engine == "t":
                banks = []
                for half in range(2):
                    bank = ps.tile([P, 1024], BF16, tag="bank", name="bank")
                    banks.append(bank)
                    for c in range(2):
                        col = 1024 * half + 512 * c
                        nc.tensor.matmul(
                            out=bank[:, 512 * c : 512 * c + 512].rearrange("p (c t) -> p c t", t=4),
                            lhsT=identb[:],
                            rhs=src[:, col : col + 512].rearrange("p (t c) -> p c t", t=4),
                            start=True,
                            stop=True,
                        )
                in_banks.append((g, banks))
                release("f", g)
                return
            if engine == "g":
                gt = slow_pool.tile([P, 2048], BF16, tag="grps", name="grp_s", align_bytes=64)
            else:
                gt = grp_pool.tile([P, 2048], BF16, tag="grp", name="grp_f", align_bytes=64)
            grouped[g] = gt
            regroup(gt[:], src, 4, engine)
            release("f", g)
            if engine == "g":
                slow.append(g)
            else:
                quantise_waiting()
                waiting.append(g)

        def feat_out_of_banks():
            if len(in_banks) == 0:
                return
            g, banks = in_banks.pop(0)
            gt = grp_pool.tile([P, 2048], BF16, tag="grp", name="grp_f", align_bytes=64)
            grouped[g] = gt
            for half in range(2):
                nc.scalar.copy(out=gt[:, 1024 * half : 1024 * half + 1024], in_=banks[half][:])
            quantise_waiting()
            waiting.append(g)

        def first_pass(h, s):
            acc = ps.tile([P, 512], F32, tag="bank", name="acc")
            nc.tensor.matmul_mx(
                out=acc[:],
                lhsT=w_codes[:, P * s : P * s + P].bitcast(FP8X4),
                lhsT_scale=w_scales[:, P * s : P * s + P],
                rhs=a_codes[:, 512 * h : 512 * h + 512].bitcast(FP8X4),
                rhs_scale=a_scales[:, 512 * h : 512 * h + 512],
                start=True,
                stop=True,
            )
            return acc

        def add_bias(xh, s, acc):
            nc.scalar.activation(
                out=xh[:].rearrange("o (v j s w) -> o v j s w", v=16, j=4, s=S)[:, :, :, s, :],
                in_=acc[:].rearrange("o (v w j) -> o v j w", v=16, j=4),
                func=ACT.Identity,
                bias=bias[:, s : s + 1],
                scale=1.0,
            )

        in2 = big.tile([P, COUT * V * 4], BF16, tag="in2", name="in2", align_bytes=64)
        in2_v = in2[:].rearrange("p (g v o j) -> p g v o j", g=32, v=V, o=4)
        pa_t = const.tile([P, V * 4], F32)

        def transposes_and_pa(h, xh, plan):
            for vl in range(16):
                v = 16 * h + vl
                tp = ps.tile([P, 512], F32, tag="bank", name="tp")
                for j in range(4):
                    col = (4 * vl + j) * P
                    nc.tensor.transpose(tp[:, P * j : P * j + P], xh[:, col : col + P], ident32[:])
                nc.vector.tensor_tensor(
                    out=in2_v[:, :, v, :, :],
                    in0=tp[:].rearrange("p (j g o) -> p g o j", j=4, o=4),
                    in1=pa_t[:, 4 * v : 4 * v + 4].unsqueeze(1).unsqueeze(1).to_broadcast([P, 32, 4, 4]),
                    op=ALU.mult,
                )
                feat_out_of_banks()
                for e in plan[vl]:
                    if e == "g" and len(slow) > 1:
                        quantise_slow()
                    feat_step(e)

        x0 = big.tile([P, 8192], F32, tag="x", name="x0")
        for e in PLAN_H:
            feat_step(e)
        if W_FIRST:
            grp_w = w_transposes(0)
            grp_a0 = regroup_a(0, "v")
            quantise(w_codes, w_scales, 0, 512, grp_w[:])
            quantise(a_codes, a_scales, 0, 512, grp_a0[:])
        else:
            grp_a0 = regroup_a(0, "v")
            quantise(a_codes, a_scales, 0, 512, grp_a0[:])
            grp_w = w_transposes(0)
            quantise(w_codes, w_scales, 0, 512, grp_w[:])
        bt = ps.tile([P, P], BF16, tag="bank", name="bt")
        nc.tensor.transpose(bt[:], b_rows[:], identb[:])
        bias = const.tile([P, S], F32)
        nc.vector.tensor_copy(out=bias[:], in_=bt[:, 0:S])
        cst = const.tile([P, 32], F32)
        bn = const.tile([P, 24], F32)
        scsh = const.tile([P, 16], F32)
        bn_rep = const.tile([P, 8 * P], BF16)
        nc.gpsimd.tensor_scalar(
            out=bn_rep[:].rearrange("p (o k) -> p o k", k=8),
            in0=bn_rows[:].unsqueeze(2).to_broadcast([P, P, 8]),
            scalar1=1.0,
            scalar2=0.0,
            op0=ALU.mult,
            op1=ALU.add,
        )
        for c in range(4):
            if c in (1, 2):
                feat_step(PLAN_W[c - 1])
            if c < 3:
                grp_w = w_transposes(c + 1)
            if c == 0:
                pt = ps.tile([P, 4 * P], BF16, tag="bank", name="pt")
                for j in range(4):
                    nc.tensor.transpose(pt[:, P * j : P * j + P], pa_rows[:, j : 512 : 4], identb[:])
            accs = [first_pass(0, s) for s in range(4 * c, 4 * c + 4)]
            if c == 0:
                nc.vector.tensor_copy(
                    out=pa_t[:].rearrange("p (v j) -> p v j", j=4),
                    in_=pt[:].rearrange("p (j v) -> p v j", j=4)[:, 0:V, :],
                )
            if c < 3:
                quantise(w_codes, w_scales, 512 * (c + 1), 512, grp_w[:])
            for s in range(4 * c, 4 * c + 4):
                add_bias(x0, s, accs[s - 4 * c])
            if c == 3:
                zt = ps.tile([P, 8 * P], BF16, tag="bank", name="zt")
                for k in range(8):
                    nc.tensor.transpose(zt[:, P * k : P * k + P], bn_rep[:, P * k : P * k + P], identb[:])
                nc.scalar.copy(
                    out=cst[:].rearrange("p (r c) -> p r c", r=4),
                    in_=zt[:].rearrange("p (c r) -> p r c", c=8)[:, 0:4, :],
                )
            if c == 3:
                grp_a1 = regroup_a(1, "v")
        quantise(a_codes, a_scales, 512, 512, grp_a1[:])
        for e in PLAN_W[2:]:
            feat_step(e)
        transposes_and_pa(0, x0, plan_t0)
        feat_out_of_banks()
        nc.gpsimd.tensor_scalar_add(out=bn[:, 0:8], in0=cst[:, 24:32], scalar1=EPS)
        nc.gpsimd.tensor_tensor(out=bn[:, 8:16], in0=bn[:, 0:8], in1=minus_half[:], op=ALU.pow)
        nc.gpsimd.tensor_tensor(out=scsh[:, 0:8], in0=cst[:, 0:8], in1=bn[:, 8:16], op=ALU.mult)
        nc.gpsimd.tensor_tensor(out=bn[:, 16:24], in0=cst[:, 16:24], in1=scsh[:, 0:8], op=ALU.mult)
        nc.gpsimd.tensor_tensor(out=scsh[:, 8:16], in0=cst[:, 8:16], in1=bn[:, 16:24], op=ALU.subtract)
        x1 = big.tile([P, 8192], F32, tag="x", name="x1")
        for s in range(S):
            add_bias(x1, s, first_pass(1, s))
            if s % 5 == 4:
                quantise_slow()
            feat_out_of_banks()
            for e in plan_s1[s]:
                feat_step(e)
        transposes_and_pa(1, x1, plan_t1)
        feat_out_of_banks()
        res_v = res.rearrange("n o v t -> (n o v t)").rearrange("(g p f) -> g p f", p=P, f=512)
        out_v = out.rearrange("n o v t -> (n o v t)").rearrange("(g p f) -> g p f", p=P, f=512)
        late = big.tile([P, 8192], F32, tag="x", name="late")
        res_tiles = {}

        def load_res(qd):
            if qd < 8:
                c0 = 6144 + 256 * qd
                r = late[:, c0 : c0 + 256].bitcast(BF16)
                nc.sync.dma_start(out=r, in_=res_v[qd])
                res_tiles[qd] = r

        def part(kind, qd):
            c0 = 2048 * kind + 512 * (qd % 4)
            return late[:, c0 : c0 + 512]

        def second_pass(ch, bank, k):
            g = ch // 4
            nc.tensor.matmul_mx(
                out=bank[:, P * k : P * k + P],
                lhsT=feat_codes(ch, 1).bitcast(FP8X4),
                lhsT_scale=f_scales[:, P * ch : P * ch + P],
                rhs=g_codes[:, P * g : P * g + P].bitcast(FP8X4),
                rhs_scale=g_scales[:, P * g : P * g + P],
                start=True,
                stop=True,
            )

        def second_passes(qd):
            for g in range(4 * qd, 4 * qd + 4):
                quantise_tile(g)
                if g in waiting:
                    waiting.remove(g)
            banks = []
            for o in range(4):
                bank = ps.tile([P, 512], F32, tag="bank", name="s2")
                banks.append(bank)
                if qd < 7:
                    for k in range(4):
                        second_pass(4 * (4 * qd + k) + o, bank, k)
            if qd == 7:
                for k in range(4):
                    for o in range(4):
                        second_pass(4 * (4 * qd + k) + o, banks[o], k)
            for o in range(4):
                dst = part(0, qd).rearrange("t (i k o b) -> t o k i b", i=4, k=4, o=4)[:, o]
                src = banks[o][:].rearrange("t (k b i o) -> t o k i b", k=4, i=4, o=4)[:, o]
                if o < Y_ON_V[qd]:
                    nc.vector.tensor_copy(out=dst, in_=src)
                else:
                    nc.scalar.copy(out=dst, in_=src)

        def halves(qd):
            return ((0, 2), (2, 4)) if qd == 7 else ((0, 4),)

        def back_and_norm(qd):
            for i0, i1 in halves(qd):
                ft = ps.tile([P, 512], F32, tag="bank", name="ft")
                for i in range(i0, i1):
                    nc.tensor.transpose(
                        ft[:, P * (i - i0) : P * (i - i0) + P], part(0, qd)[:, P * i : P * i + P], ident32[:]
                    )
                nc.vector.scalar_tensor_tensor(
                    out=part(1, qd)[:, P * i0 : P * i1],
                    in0=ft[:, 0 : P * (i1 - i0)],
                    scalar=scsh[:, qd : qd + 1],
                    in1=res_tiles[qd][:, P * i0 : P * i1],
                    op0=ALU.mult,
                    op1=ALU.add,
                )

        def relu_and_store(qd):
            for i0, i1 in halves(qd):
                z = part(1, qd)[:, P * i0 : P * i1]
                r = part(2, qd)[:, P * i0 : P * i1]
                if qd >= RELU_S:
                    nc.scalar.activation(out=r, in_=z, func=ACT.Relu, bias=scsh[:, 8 + qd : 9 + qd], scale=1.0)
                else:
                    nc.vector.tensor_scalar(
                        out=r,
                        in0=z,
                        scalar1=scsh[:, 8 + qd : 9 + qd],
                        scalar2=0.0,
                        op0=ALU.add,
                        op1=ALU.max,
                    )
                nc.sync.dma_start(out=out_v[qd][:, P * i0 : P * i1], in_=r)

        for qd in range(AHEAD):
            load_res(qd)
        g_codes = big.tile([P, COUT * V], U32, tag="g", name="g_codes", align_bytes=64)
        for i in range(9 + LAG + 1):
            if i < 4:
                quantise(g_codes, g_scales, 1024 * i, 1024, in2[:, 4096 * i : 4096 * i + 4096])
                quantise_slow()
            feat_out_of_banks()
            if 1 <= i < 9:
                second_passes(i - 1)
            if i > len(PLAN_TAIL):
                quantise_waiting()
            if 1 + LAG <= i < 9 + LAG:
                back_and_norm(i - LAG - 1)
            if i > LAG + 1:
                relu_and_store(i - LAG - 2)
            load_res(i + AHEAD)
            if i < len(PLAN_TAIL):
                for e in PLAN_TAIL[i]:
                    feat_step(e)
